import numpy as np
import ml_dtypes


def mxq(x, axis, fmt="e4m3"):
    dtype, down = {"e4m3": (ml_dtypes.float8_e4m3fn, 7), "e5m2": (ml_dtypes.float8_e5m2, 14)}[fmt]
    v = np.moveaxis(np.asarray(x, np.float32).astype(ml_dtypes.bfloat16).astype(np.float64), axis, -1)
    blocks = v.reshape(v.shape[:-1] + (-1, 32))
    amax = np.abs(blocks).max(-1, keepdims=True)
    byte = np.maximum(np.where(amax > 0, np.frexp(amax)[1] - 1 + 127, 0) - down, 1)
    scale = np.exp2(byte - 127.0)
    codes = (blocks / scale).astype(np.float32).astype(dtype).astype(np.float64)
    return np.moveaxis((codes * scale).reshape(v.shape), -1, axis)


WIDE = False


def mx_kscale(k):
    if not WIDE:
        return np.ones(k)
    levels = np.array([10, -10, 5, -5, 0])
    if k % 512:
        return np.exp2(np.random.permutation(np.resize(levels, k // 32))).repeat(32)
    a = np.empty((k // 512, 16))
    for p in range(k // 512):
        a[p, :8] = np.random.permutation(np.resize(levels, 8))
        for g in range(8):
            far = levels[np.abs(levels - a[p, g]) >= 10]
            a[p, g + 8] = far[np.random.randint(len(far))]
    return np.exp2(a.ravel()).repeat(32)


BF16 = ml_dtypes.bfloat16


def bf(x):
    return np.asarray(x, np.float32).astype(BF16)


def f64(x):
    return np.asarray(x).astype(np.float64)


B, NV, S, D, H = 2, 8, 128, 1024, 8
HD = D // H


def setup_inputs():
    s, t = mx_kscale(D), mx_kscale(D)
    return {"x": bf(np.random.standard_normal((B * NV, S, D)) * s),
            "scores": bf(np.random.standard_normal((B, NV, NV, H, S)) * 1.4),
            "Wv": bf(np.random.standard_normal((D, D)) / np.sqrt(D) / s[:, None] * t),
            "bv": bf(np.random.standard_normal(D) * 0.3 * t),
            "Wo": bf(np.random.standard_normal((D, D)) / np.sqrt(D) / t[:, None]),
            "bo": bf(np.random.standard_normal(D) * 0.3)}


def reference(x, scores, Wv, bv, Wo, bo):
    v = (mxq(f64(x), 2, "e4m3") @ mxq(f64(Wv), 0, "e4m3")) + f64(bv)
    v = v.reshape(B, NV, S, H, HD).transpose(0, 1, 3, 2, 4)
    sc = f64(scores)
    e = np.exp(sc - sc.max(2, keepdims=True))
    w = e / e.sum(2, keepdims=True)
    mixed = np.zeros((B, NV, H, S, HD))
    for j in range(NV):
        mixed = mixed + w[:, :, j, :, :, None] * v[:, j][:, None]
    mixed = mixed.transpose(0, 1, 3, 2, 4).reshape(B * NV, S, D)
    return (mxq(mixed, 2, "e4m3") @ mxq(f64(Wo), 0, "e4m3")) + f64(bo)

@@ -1,0 +1,380 @@
+from contextlib import ExitStack
+
+import concourse.mybir as mybir
+from concourse.masks import make_identity
+
+F32 = mybir.dt.float32
+BF16 = mybir.dt.bfloat16
+U32 = mybir.dt.uint32
+U8 = mybir.dt.uint8
+FP8X4 = mybir.dt.float8_e4m3fn_x4
+ADD = mybir.AluOpType.add
+SUBTRACT = mybir.AluOpType.subtract
+MULT = mybir.AluOpType.mult
+MAX = mybir.AluOpType.max
+INNERMOST = mybir.AxisListType.X
+EXP = mybir.ActivationFunctionType.Exp
+
+P = 128
+SCENES, VIEWS, POSITIONS, FEATURES, HEADS = 2, 8, 128, 1024, 8
+PACK = 4
+K_PASS = P * PACK
+PASSES = FEATURES // K_PASS
+N_TILE = 512
+N_HALVES = FEATURES // N_TILE
+GROUP_POS = P // VIEWS
+CHUNKS = POSITIONS // GROUP_POS
+GROUPS = SCENES * CHUNKS
+
+PIECE_CHUNKS = 2
+PIECE_GROUPS = PIECE_CHUNKS * SCENES
+PIECE_POS = PIECE_CHUNKS * GROUP_POS
+PIECES = CHUNKS // PIECE_CHUNKS
+
+AHEAD_V = 2
+AHEAD_X = 2
+AHEAD_W = 2
+BEHIND_Y = 3
+FIRST_STEP = -(AHEAD_W + 3)
+
+FLOPS = 2 * 2 * SCENES * VIEWS * POSITIONS * FEATURES * FEATURES + 2 * SCENES * VIEWS * VIEWS * POSITIONS * FEATURES
+
+
+def tile_crossviewattention_pa_kernel(tc, x, scores, Wv, bv, Wo, bo, out):
+    nc = tc.nc
+    with ExitStack() as ctx:
+        keep = ctx.enter_context(tc.tile_pool(name="keep", bufs=1))
+        x_stage = ctx.enter_context(tc.tile_pool(name="x_stage", bufs=3))
+        w_stage = ctx.enter_context(tc.tile_pool(name="w_stage", bufs=4))
+        s_pool = ctx.enter_context(tc.tile_pool(name="s_pool", bufs=2))
+        v_pool = ctx.enter_context(tc.tile_pool(name="v_pool", bufs=AHEAD_V + 2))
+        mixw_pool = ctx.enter_context(tc.tile_pool(name="mixw_pool", bufs=AHEAD_W + 2))
+        m_pool = ctx.enter_context(tc.tile_pool(name="m_pool", bufs=BEHIND_Y + 2))
+        y_pool = ctx.enter_context(tc.tile_pool(name="y_pool", bufs=6))
+        psum = ctx.enter_context(tc.psum_pool(name="psum", bufs=2))
+        ctx.enter_context(tc.manual_schedule())
+
+        def chunk_and_scene(grp):
+            return divmod(grp, SCENES)
+
+        def group_rows(dram, grp, cols):
+            c, b = chunk_and_scene(grp)
+            block = dram[b * VIEWS : (b + 1) * VIEWS, c * GROUP_POS : (c + 1) * GROUP_POS, cols]
+            return block.rearrange("j s k -> s j k")
+
+        def half_cols(half):
+            return slice(half * N_TILE, (half + 1) * N_TILE)
+
+        x_raw = keep.tile([P, GROUPS, FEATURES], BF16)
+        x_codes = keep.tile([P, GROUPS, PASSES * P], U32, align_bytes=64)
+        x_scales = keep.tile([P, GROUPS, PASSES * P], U8, align_bytes=64)
+        wv_raw = keep.tile([P, PASSES, PACK, FEATURES], BF16)
+        wv_codes = keep.tile([P, PASSES, FEATURES], U32, align_bytes=64)
+        wv_scales = keep.tile([P, PASSES, FEATURES], U8, align_bytes=64)
+        wo_raw = keep.tile([P, PASSES, PACK, FEATURES], BF16)
+        wo_codes = keep.tile([P, PASSES, FEATURES], U32, align_bytes=64)
+        wo_scales = keep.tile([P, PASSES, FEATURES], U8, align_bytes=64)
+        score_raw = keep.tile([P, VIEWS, POSITIONS], BF16)
+        bv_all = keep.tile([P, FEATURES], BF16)
+        bo_all = keep.tile([P, FEATURES], BF16)
+
+        def load_tokens(grp):
+            nc.sync.dma_start(out=x_raw[:, grp, :], in_=group_rows(x, grp, slice(0, FEATURES)))
+
+        def load_wv(g):
+            nc.sync.dma_start(
+                out=wv_raw[:, g, :, :],
+                in_=Wv[g * K_PASS : (g + 1) * K_PASS, :].rearrange("(p t) n -> p t n", t=PACK),
+            )
+
+        def load_wo(g):
+            nc.sync.dma_start(
+                out=wo_raw[:, g, :, :],
+                in_=Wo[g * K_PASS : (g + 1) * K_PASS, :].rearrange("(p t) n -> p t n", t=PACK),
+            )
+
+        def load_scores(j):
+            nc.scalar.dma_start(
+                out=score_raw[:, j, :], in_=scores[:, :, j, :, :].rearrange("b i h s -> (b i) h s")
+            )
+
+        for j in range(VIEWS - 2):
+            load_scores(j)
+        load_tokens(0)
+        load_wv(0)
+        for j in range(VIEWS - 2, VIEWS):
+            load_scores(j)
+        load_wv(1)
+        for grp in range(1, AHEAD_V + AHEAD_X):
+            load_tokens(grp)
+        for g in range(PASSES):
+            load_wo(g)
+        for grp in range(AHEAD_V + AHEAD_X, GROUPS):
+            load_tokens(grp)
+        nc.sync.dma_start(out=bv_all[:], in_=bv.partition_broadcast(P))
+        nc.sync.dma_start(out=bo_all[:], in_=bo.partition_broadcast(P))
+
+        ident = keep.tile([P, P], F32)
+        make_identity(nc, ident[:])
+        same_pos = keep.tile([P, GROUP_POS], F32)
+        nc.vector.tensor_reduce(
+            out=same_pos[:], in_=ident[:].rearrange("p (s i) -> p s i", i=VIEWS), axis=INNERMOST, op=ADD
+        )
+        block_mask = keep.tile([P, GROUP_POS, VIEWS], F32)
+        nc.vector.tensor_copy(
+            out=block_mask[:], in_=same_pos[:].unsqueeze(2).to_broadcast([P, GROUP_POS, VIEWS])
+        )
+
+        grouped_weights = {}
+
+        def regroup_weights(name, raw, g):
+            for half, copy in enumerate((nc.vector.tensor_copy, nc.scalar.copy)):
+                grouped_w = w_stage.tile([P, N_TILE, PACK], BF16, align_bytes=64)
+                copy(
+                    out=grouped_w[:].rearrange("p (c i) t -> p c t i", i=4),
+                    in_=raw[:, g, :, half_cols(half)].rearrange("p t (c i) -> p c t i", i=4),
+                )
+                grouped_weights[(name, g, half)] = grouped_w
+
+        def quantise_weights(name, codes, scales, g):
+            for half in range(N_HALVES):
+                nc.vector.quantize_mx(
+                    out=codes[:, g, half_cols(half)].bitcast(FP8X4),
+                    scales=scales[:, g, half_cols(half)],
+                    in_=grouped_weights[(name, g, half)][:].rearrange("p n t -> p (n t)"),
+                )
+
+        grouped_tokens = {}
+
+        def transpose_tokens(grp):
+            words = x_raw[:, grp, :].bitcast(F32)
+            flipped = psum.tile([P, PACK, P], F32, tag="flip")
+            for g in range(PASSES):
+                for u in range(2):
+                    nc.tensor.transpose(
+                        flipped[:, 2 * g + u, :], words[:, 2 * P * g + u : 2 * P * (g + 1) : 2], ident[:]
+                    )
+            grouped_x = x_stage.tile([P, PASSES, P, PACK], BF16, align_bytes=64)
+            nc.scalar.copy(
+                out=grouped_x[:].bitcast(F32), in_=flipped[:].rearrange("p (g u) n -> p g n u", u=2)
+            )
+            grouped_tokens[grp] = grouped_x
+
+        def quantise_tokens(grp):
+            nc.vector.quantize_mx(
+                out=x_codes[:, grp, :].bitcast(FP8X4),
+                scales=x_scales[:, grp, :],
+                in_=grouped_tokens[grp][:].rearrange("p g n t -> p (g n t)"),
+            )
+
+        weights_t = keep.tile([P, CHUNKS, SCENES, HEADS, VIEWS], F32)
+        piece_shape = [P, PIECE_POS, VIEWS]
+        exponents = {}
+        piece_weights = {}
+
+        def softmax_shift(piece):
+            by_pos = score_raw[:, :, piece * PIECE_POS : (piece + 1) * PIECE_POS].rearrange("p j s -> p s j")
+            top = s_pool.tile([P, PIECE_POS], F32)
+            nc.vector.tensor_reduce(out=top[:], in_=by_pos, axis=INNERMOST, op=MAX)
+            expd = s_pool.tile(piece_shape, F32)
+            nc.vector.tensor_tensor(
+                out=expd[:], in0=by_pos, in1=top[:].unsqueeze(2).to_broadcast(piece_shape), op=SUBTRACT
+            )
+            exponents[piece] = expd
+
+        def softmax_exp(piece):
+            nc.scalar.activation(out=exponents[piece][:], in_=exponents[piece][:], func=EXP)
+
+        def softmax_normalise(piece):
+            total = s_pool.tile([P, PIECE_POS], F32)
+            nc.vector.tensor_reduce(out=total[:], in_=exponents[piece][:], axis=INNERMOST, op=ADD)
+            inverse = s_pool.tile([P, PIECE_POS], F32)
+            nc.vector.reciprocal(out=inverse[:], in_=total[:])
+            weights = s_pool.tile([P, PIECE_CHUNKS, P], F32)
+            nc.vector.tensor_tensor(
+                out=weights[:].rearrange("p c (s j) -> p (c s) j", j=VIEWS),
+                in0=exponents[piece][:],
+                in1=inverse[:].unsqueeze(2).to_broadcast(piece_shape),
+                op=MULT,
+            )
+            piece_weights[piece] = weights
+
+        def softmax_transpose(piece):
+            flipped = psum.tile([P, PACK, P], F32, tag="flip")
+            for c in range(PIECE_CHUNKS):
+                nc.tensor.transpose(flipped[:, c, :], piece_weights[piece][:, c, :], ident[:])
+            chunks = slice(piece * PIECE_CHUNKS, (piece + 1) * PIECE_CHUNKS)
+            nc.scalar.copy(
+                out=weights_t[:, chunks].rearrange("p c b h i -> p (c b) h i"),
+                in_=flipped[:, 0:PIECE_CHUNKS, :].rearrange("p c (b i h) -> p (c b) h i", b=SCENES, i=VIEWS),
+            )
+
+        def piece_that_starts_at(grp):
+            piece, offset = divmod(grp, PIECE_GROUPS)
+            return piece if offset == 0 and 0 <= piece < PIECES else None
+
+        values = {}
+        mix_weights = {}
+        mix_sums = {}
+        mixed_tokens = {}
+        grouped_mixed = {}
+        mixed_codes = {}
+        out_sums = {}
+
+        def first_projection(grp):
+            v_rows = v_pool.tile([P, FEATURES], F32)
+            for half in range(N_HALVES):
+                acc = psum.tile([P, N_TILE], F32, tag="acc_v")
+                for g in range(PASSES):
+                    toks = slice(g * P, (g + 1) * P)
+                    nc.tensor.matmul_mx(
+                        out=acc[:],
+                        lhsT=x_codes[:, grp, toks].bitcast(FP8X4),
+                        lhsT_scale=x_scales[:, grp, toks],
+                        rhs=wv_codes[:, g, half_cols(half)].bitcast(FP8X4),
+                        rhs_scale=wv_scales[:, g, half_cols(half)],
+                        start=(g == 0),
+                        stop=(g == PASSES - 1),
+                    )
+                nc.scalar.copy(out=v_rows[:, half_cols(half)], in_=acc[:])
+            values[grp] = v_rows
+
+        def build_mix_weights(grp):
+            c, b = chunk_and_scene(grp)
+            shape = [P, HEADS, GROUP_POS, VIEWS]
+            mixw = mixw_pool.tile(shape, F32)
+            nc.gpsimd.tensor_tensor(
+                out=mixw[:],
+                in0=weights_t[:, c, b, :, :].unsqueeze(2).to_broadcast(shape),
+                in1=block_mask[:].unsqueeze(1).to_broadcast(shape),
+                op=MULT,
+            )
+            mix_weights[grp] = mixw
+
+        def mix(grp):
+            sums = []
+            for g in range(PASSES):
+                acc = psum.tile([P, PACK, P], F32, tag="acc_mix")
+                for t in range(PACK):
+                    h = g * PACK + t
+                    nc.tensor.matmul(
+                        out=acc[:, t, :],
+                        lhsT=mix_weights[grp][:, h, :, :].rearrange("p s i -> p (s i)"),
+                        rhs=values[grp][:, h * P : (h + 1) * P],
+                        start=True,
+                        stop=True,
+                    )
+                sums.append(acc)
+            mix_sums[grp] = sums
+
+        def round_mixed(grp):
+            mixed = m_pool.tile([P, PASSES, 2, P, 2], BF16, align_bytes=64)
+            for g in range(PASSES):
+                nc.vector.tensor_tensor(
+                    out=mixed[:, g],
+                    in0=mix_sums[grp][g][:].rearrange("p t f -> p (t f)").rearrange("p (q u e) -> p u q e", u=2, e=2),
+                    in1=bv_all[:, g * K_PASS : (g + 1) * K_PASS].rearrange("p (q u e) -> p u q e", u=2, e=2),
+                    op=ADD,
+                )
+            mixed_tokens[grp] = mixed
+
+        def transpose_mixed(grp):
+            words = mixed_tokens[grp][:].rearrange("p g u q e -> p (g u q e)").bitcast(F32)
+            flipped = psum.tile([P, PACK, P], F32, tag="flip")
+            for c in range(PACK):
+                nc.tensor.transpose(flipped[:, c, :], words[:, c * P : (c + 1) * P], ident[:])
+            grouped_m = m_pool.tile([P, PASSES, P, PACK], BF16, align_bytes=64)
+            nc.scalar.copy(
+                out=grouped_m[:].bitcast(F32), in_=flipped[:].rearrange("p (g u) n -> p g n u", u=2)
+            )
+            grouped_mixed[grp] = grouped_m
+
+        def quantise_mixed(grp):
+            m_codes = m_pool.tile([P, PASSES * P], U32, align_bytes=64)
+            m_scales = m_pool.tile([P, PASSES * P], U8, align_bytes=64)
+            nc.vector.quantize_mx(
+                out=m_codes[:].bitcast(FP8X4),
+                scales=m_scales[:],
+                in_=grouped_mixed[grp][:].rearrange("p g n t -> p (g n t)"),
+            )
+            mixed_codes[grp] = (m_codes, m_scales)
+
+        def second_projection(grp):
+            m_codes, m_scales = mixed_codes[grp]
+            sums = []
+            for half in range(N_HALVES):
+                acc = psum.tile([P, N_TILE], F32, tag="acc_y")
+                for g in range(PASSES):
+                    toks = slice(g * P, (g + 1) * P)
+                    nc.tensor.matmul_mx(
+                        out=acc[:],
+                        lhsT=m_codes[:, toks].bitcast(FP8X4),
+                        lhsT_scale=m_scales[:, toks],
+                        rhs=wo_codes[:, g, half_cols(half)].bitcast(FP8X4),
+                        rhs_scale=wo_scales[:, g, half_cols(half)],
+                        start=(g == 0),
+                        stop=(g == PASSES - 1),
+                    )
+                sums.append(acc)
+            out_sums[grp] = sums
+
+        def finish(grp):
+            for half in range(N_HALVES):
+                result = y_pool.tile([P, N_TILE], F32)
+                nc.vector.tensor_tensor(
+                    out=result[:], in0=out_sums[grp][half][:], in1=bo_all[:, half_cols(half)], op=ADD
+                )
+                nc.sync.dma_start(out=group_rows(out, grp, half_cols(half)), in_=result[:])
+
+        def is_group(grp):
+            return 0 <= grp < GROUPS
+
+        def is_pass(g):
+            return 0 <= g < PASSES
+
+        wv_start = -(AHEAD_V + AHEAD_X)
+        wo_start = BEHIND_Y - PASSES - 1
+        for step in range(FIRST_STEP, GROUPS + BEHIND_Y):
+            if is_group(step - 1):
+                round_mixed(step - 1)
+            if is_group(step - BEHIND_Y):
+                second_projection(step - BEHIND_Y)
+                finish(step - BEHIND_Y)
+            if is_group(step - 2):
+                quantise_mixed(step - 2)
+            if is_pass(step - wv_start - 1):
+                quantise_weights("wv", wv_codes, wv_scales, step - wv_start - 1)
+            if is_pass(step - wo_start - 1):
+                quantise_weights("wo", wo_codes, wo_scales, step - wo_start - 1)
+            if is_group(step + AHEAD_V):
+                first_projection(step + AHEAD_V)
+
+            piece = piece_that_starts_at(step + AHEAD_W + 2)
+            if piece is not None:
+                softmax_exp(piece)
+            if is_pass(step - wv_start):
+                regroup_weights("wv", wv_raw, step - wv_start)
+            if is_pass(step - wo_start):
+                regroup_weights("wo", wo_raw, step - wo_start)
+
+            if is_group(step + AHEAD_V + AHEAD_X):
+                transpose_tokens(step + AHEAD_V + AHEAD_X)
+            if is_group(step - 1):
+                transpose_mixed(step - 1)
+            piece = piece_that_starts_at(step + AHEAD_W + 1)
+            if piece is not None:
+                softmax_transpose(piece)
+            if is_group(step + AHEAD_V + AHEAD_X - 1):
+                quantise_tokens(step + AHEAD_V + AHEAD_X - 1)
+
+            piece = piece_that_starts_at(step + AHEAD_W + 2)
+            if piece is not None:
+                softmax_normalise(piece)
+            piece = piece_that_starts_at(step + AHEAD_W + 3)
+            if piece is not None:
+                softmax_shift(piece)
+
+            if is_group(step + AHEAD_W):
+                build_mix_weights(step + AHEAD_W)
+            if is_group(step):
+                mix(step)

@@ -22,6 +22,7 @@ K_PASS = P * PACK
 PASSES = FEATURES // K_PASS
 N_TILE = 512
 N_HALVES = FEATURES // N_TILE
+N_QUARTER = N_TILE // 2
 GROUP_POS = P // VIEWS
 CHUNKS = POSITIONS // GROUP_POS
 GROUPS = SCENES * CHUNKS
@@ -30,12 +31,19 @@ PIECE_CHUNKS = 2
 PIECE_GROUPS = PIECE_CHUNKS * SCENES
 PIECE_POS = PIECE_CHUNKS * GROUP_POS
 PIECES = CHUNKS // PIECE_CHUNKS
+SLAB_GROUPS = 2
+SLABS = GROUPS // SLAB_GROUPS
+TURNED_BY_TENSOR = 4
+FIRST_SLAB = TURNED_BY_TENSOR // SLAB_GROUPS
+QUADS = 4
+QUAD = P // QUADS
+QUAD_FEATURES = K_PASS // QUADS
 
-AHEAD_V = 2
-AHEAD_X = 2
+AHEAD_V = 1
 AHEAD_W = 2
 BEHIND_Y = 3
-FIRST_STEP = -(AHEAD_W + 3)
+FIRST_STEP = -AHEAD_V
+MIX_HEADS = 2
 
 FLOPS = 2 * 2 * SCENES * VIEWS * POSITIONS * FEATURES * FEATURES + 2 * SCENES * VIEWS * VIEWS * POSITIONS * FEATURES
 
@@ -55,7 +63,9 @@ def tile_crossviewattention_pa_kernel(tc, x, scores, Wv, bv, Wo, bo, out):
         ctx.enter_context(tc.manual_schedule())
 
         def chunk_and_scene(grp):
-            return divmod(grp, SCENES)
+            piece, rest = divmod(grp, PIECE_GROUPS)
+            b, part = divmod(rest, PIECE_CHUNKS)
+            return piece * PIECE_CHUNKS + part, b
 
         def group_rows(dram, grp, cols):
             c, b = chunk_and_scene(grp)
@@ -65,7 +75,8 @@ def tile_crossviewattention_pa_kernel(tc, x, scores, Wv, bv, Wo, bo, out):
         def half_cols(half):
             return slice(half * N_TILE, (half + 1) * N_TILE)
 
-        x_raw = keep.tile([P, GROUPS, FEATURES], BF16)
+        x_rows = keep.tile([P, TURNED_BY_TENSOR, FEATURES], BF16)
+        x_slabs = keep.tile([P, SLABS - FIRST_SLAB, VIEWS, PASSES, QUAD_FEATURES], BF16)
         x_codes = keep.tile([P, GROUPS, PASSES * P], U32, align_bytes=64)
         x_scales = keep.tile([P, GROUPS, PASSES * P], U8, align_bytes=64)
         wv_raw = keep.tile([P, PASSES, PACK, FEATURES], BF16)
@@ -79,12 +90,23 @@ def tile_crossviewattention_pa_kernel(tc, x, scores, Wv, bv, Wo, bo, out):
         bo_all = keep.tile([P, FEATURES], BF16)
 
         def load_tokens(grp):
-            nc.sync.dma_start(out=x_raw[:, grp, :], in_=group_rows(x, grp, slice(0, FEATURES)))
+            nc.sync.dma_start(out=x_rows[:, grp, :], in_=group_rows(x, grp, slice(0, FEATURES)))
 
-        def load_wv(g):
+        def load_slab(slab):
+            piece, b = divmod(slab, SCENES)
+            block = x[b * VIEWS : (b + 1) * VIEWS, piece * PIECE_POS : (piece + 1) * PIECE_POS, :]
+            for g in range(PASSES):
+                for a in range(QUADS):
+                    first = g * K_PASS + a * QUAD_FEATURES
+                    nc.sync.dma_start(
+                        out=x_slabs[a * QUAD : (a + 1) * QUAD, slab - FIRST_SLAB, :, g, :],
+                        in_=block[:, :, first : first + QUAD_FEATURES].rearrange("j r k -> r j k"),
+                    )
+
+        def load_wv(g, half):
             nc.sync.dma_start(
-                out=wv_raw[:, g, :, :],
-                in_=Wv[g * K_PASS : (g + 1) * K_PASS, :].rearrange("(p t) n -> p t n", t=PACK),
+                out=wv_raw[:, g, :, half_cols(half)],
+                in_=Wv[g * K_PASS : (g + 1) * K_PASS, half_cols(half)].rearrange("(p t) n -> p t n", t=PACK),
             )
 
         def load_wo(g):
@@ -98,24 +120,27 @@ def tile_crossviewattention_pa_kernel(tc, x, scores, Wv, bv, Wo, bo, out):
                 out=score_raw[:, j, :], in_=scores[:, :, j, :, :].rearrange("b i h s -> (b i) h s")
             )
 
-        for j in range(VIEWS - 2):
-            load_scores(j)
-        load_tokens(0)
-        load_wv(0)
-        for j in range(VIEWS - 2, VIEWS):
-            load_scores(j)
-        load_wv(1)
-        for grp in range(1, AHEAD_V + AHEAD_X):
-            load_tokens(grp)
-        for g in range(PASSES):
-            load_wo(g)
-        for grp in range(AHEAD_V + AHEAD_X, GROUPS):
-            load_tokens(grp)
-        nc.sync.dma_start(out=bv_all[:], in_=bv.partition_broadcast(P))
-        nc.sync.dma_start(out=bo_all[:], in_=bo.partition_broadcast(P))
-
         ident = keep.tile([P, P], F32)
         make_identity(nc, ident[:])
+
+        load_tokens(0)
+        for j in range(5):
+            load_scores(j)
+        for g in range(PASSES):
+            load_wv(g, 0)
+        for j in range(5, VIEWS):
+            load_scores(j)
+        for g in range(PASSES):
+            load_wv(g, 1)
+        for grp in range(1, TURNED_BY_TENSOR):
+            load_tokens(grp)
+        load_slab(FIRST_SLAB)
+        nc.sync.dma_start(out=bv_all[:], in_=bv.partition_broadcast(P))
+        for g in range(PASSES):
+            load_wo(g)
+        nc.sync.dma_start(out=bo_all[:], in_=bo.partition_broadcast(P))
+        for slab in range(FIRST_SLAB + 1, SLABS):
+            load_slab(slab)
         same_pos = keep.tile([P, GROUP_POS], F32)
         nc.vector.tensor_reduce(
             out=same_pos[:], in_=ident[:].rearrange("p (s i) -> p s i", i=VIEWS), axis=INNERMOST, op=ADD
@@ -127,27 +152,37 @@ def tile_crossviewattention_pa_kernel(tc, x, scores, Wv, bv, Wo, bo, out):
 
         grouped_weights = {}
 
-        def regroup_weights(name, raw, g):
-            for half, copy in enumerate((nc.vector.tensor_copy, nc.scalar.copy)):
+        def regroup_weights(copy, name, raw, g, quarter):
+            half, part = divmod(quarter, 2)
+            key = (name, g, half)
+            if key not in grouped_weights:
                 grouped_w = w_stage.tile([P, N_TILE, PACK], BF16, align_bytes=64)
-                copy(
-                    out=grouped_w[:].rearrange("p (c i) t -> p c t i", i=4),
-                    in_=raw[:, g, :, half_cols(half)].rearrange("p t (c i) -> p c t i", i=4),
-                )
-                grouped_weights[(name, g, half)] = grouped_w
+                grouped_weights[key] = grouped_w
+            inner = slice(part * N_QUARTER, (part + 1) * N_QUARTER)
+            outer = slice(quarter * N_QUARTER, (quarter + 1) * N_QUARTER)
+            copy(
+                out=grouped_weights[key][:, inner, :].rearrange("p (c i) t -> p c t i", i=4),
+                in_=raw[:, g, :, outer].rearrange("p t (c i) -> p c t i", i=4),
+            )
 
-        def quantise_weights(name, codes, scales, g):
-            for half in range(N_HALVES):
-                nc.vector.quantize_mx(
-                    out=codes[:, g, half_cols(half)].bitcast(FP8X4),
-                    scales=scales[:, g, half_cols(half)],
-                    in_=grouped_weights[(name, g, half)][:].rearrange("p n t -> p (n t)"),
-                )
+        def quantise_weights(name, codes, scales, g, half):
+            nc.vector.quantize_mx(
+                out=codes[:, g, half_cols(half)].bitcast(FP8X4),
+                scales=scales[:, g, half_cols(half)],
+                in_=grouped_weights[(name, g, half)][:].rearrange("p n t -> p (n t)"),
+            )
+
+        def regroup_wv(copy, g, quarter):
+            regroup_weights(copy, "wv", wv_raw, g, quarter)
+
+        def regroup_wo(g, half):
+            regroup_weights(nc.vector.tensor_copy, "wo", wo_raw, g, 2 * half)
+            regroup_weights(nc.scalar.copy, "wo", wo_raw, g, 2 * half + 1)
 
         grouped_tokens = {}
 
         def transpose_tokens(grp):
-            words = x_raw[:, grp, :].bitcast(F32)
+            words = x_rows[:, grp, :].bitcast(F32)
             flipped = psum.tile([P, PACK, P], F32, tag="flip")
             for g in range(PASSES):
                 for u in range(2):
@@ -158,6 +193,37 @@ def tile_crossviewattention_pa_kernel(tc, x, scores, Wv, bv, Wo, bo, out):
             nc.scalar.copy(
                 out=grouped_x[:].bitcast(F32), in_=flipped[:].rearrange("p (g u) n -> p g n u", u=2)
             )
+            grouped_tokens[grp] = grouped_x
+
+        ordered_slabs = {}
+        turned_slabs = {}
+
+        def order_slab(slab):
+            ordered = x_stage.tile([P, VIEWS, PASSES, 2, QUAD], F32, align_bytes=64)
+            words = x_slabs[:, slab - FIRST_SLAB].rearrange("p j g k -> p (j g k)").bitcast(F32)
+            nc.scalar.copy(
+                out=ordered[:].rearrange("p j g u i -> p (j g) u i"),
+                in_=words.rearrange("p (b i u) -> p b u i", i=QUAD, u=2),
+            )
+            ordered_slabs[slab] = ordered
+
+        def turn_slab(slab):
+            turned = x_stage.tile([P, VIEWS, PASSES, 2, QUAD], F32, align_bytes=64)
+            nc.vector.transpose(
+                out=turned[:].rearrange("p j g u r -> p (j g u r)"),
+                in_=ordered_slabs[slab][:].rearrange("p j g u i -> p (j g u i)"),
+            )
+            turned_slabs[slab] = turned
+
+        def group_tokens(grp):
+            slab, part = divmod(grp, SLAB_GROUPS)
+            grouped_x = x_stage.tile([P, PASSES, P, PACK], BF16, align_bytes=64)
+            positions = slice(part * GROUP_POS, (part + 1) * GROUP_POS)
+            for g in range(PASSES):
+                nc.scalar.copy(
+                    out=grouped_x[:, g, :, :].bitcast(F32).rearrange("p (s j) u -> p s j u", j=VIEWS),
+                    in_=turned_slabs[slab][:, :, g, :, positions].rearrange("p j u s -> p s j u"),
+                )
             grouped_tokens[grp] = grouped_x
 
         def quantise_tokens(grp):
@@ -177,7 +243,7 @@ def tile_crossviewattention_pa_kernel(tc, x, scores, Wv, bv, Wo, bo, out):
             top = s_pool.tile([P, PIECE_POS], F32)
             nc.vector.tensor_reduce(out=top[:], in_=by_pos, axis=INNERMOST, op=MAX)
             expd = s_pool.tile(piece_shape, F32)
-            nc.vector.tensor_tensor(
+            nc.gpsimd.tensor_tensor(
                 out=expd[:], in0=by_pos, in1=top[:].unsqueeze(2).to_broadcast(piece_shape), op=SUBTRACT
             )
             exponents[piece] = expd
@@ -191,7 +257,7 @@ def tile_crossviewattention_pa_kernel(tc, x, scores, Wv, bv, Wo, bo, out):
             inverse = s_pool.tile([P, PIECE_POS], F32)
             nc.vector.reciprocal(out=inverse[:], in_=total[:])
             weights = s_pool.tile([P, PIECE_CHUNKS, P], F32)
-            nc.vector.tensor_tensor(
+            nc.gpsimd.tensor_tensor(
                 out=weights[:].rearrange("p c (s j) -> p (c s) j", j=VIEWS),
                 in0=exponents[piece][:],
                 in1=inverse[:].unsqueeze(2).to_broadcast(piece_shape),
@@ -221,34 +287,35 @@ def tile_crossviewattention_pa_kernel(tc, x, scores, Wv, bv, Wo, bo, out):
         mixed_codes = {}
         out_sums = {}
 
-        def first_projection(grp):
-            v_rows = v_pool.tile([P, FEATURES], F32)
-            for half in range(N_HALVES):
-                acc = psum.tile([P, N_TILE], F32, tag="acc_v")
-                for g in range(PASSES):
-                    toks = slice(g * P, (g + 1) * P)
-                    nc.tensor.matmul_mx(
-                        out=acc[:],
-                        lhsT=x_codes[:, grp, toks].bitcast(FP8X4),
-                        lhsT_scale=x_scales[:, grp, toks],
-                        rhs=wv_codes[:, g, half_cols(half)].bitcast(FP8X4),
-                        rhs_scale=wv_scales[:, g, half_cols(half)],
-                        start=(g == 0),
-                        stop=(g == PASSES - 1),
-                    )
-                nc.scalar.copy(out=v_rows[:, half_cols(half)], in_=acc[:])
-            values[grp] = v_rows
+        def first_projection(grp, half):
+            if half == 0:
+                v_rows = v_pool.tile([P, FEATURES], F32)
+                values[grp] = v_rows
+            acc = psum.tile([P, N_TILE], F32, tag="acc_v")
+            for g in range(PASSES):
+                toks = slice(g * P, (g + 1) * P)
+                nc.tensor.matmul_mx(
+                    out=acc[:],
+                    lhsT=x_codes[:, grp, toks].bitcast(FP8X4),
+                    lhsT_scale=x_scales[:, grp, toks],
+                    rhs=wv_codes[:, g, half_cols(half)].bitcast(FP8X4),
+                    rhs_scale=wv_scales[:, g, half_cols(half)],
+                    start=(g == 0),
+                    stop=(g == PASSES - 1),
+                )
+            nc.scalar.copy(out=values[grp][:, half_cols(half)], in_=acc[:])
 
         def build_mix_weights(grp):
             c, b = chunk_and_scene(grp)
-            shape = [P, HEADS, GROUP_POS, VIEWS]
-            mixw = mixw_pool.tile(shape, F32)
-            nc.gpsimd.tensor_tensor(
-                out=mixw[:],
-                in0=weights_t[:, c, b, :, :].unsqueeze(2).to_broadcast(shape),
-                in1=block_mask[:].unsqueeze(1).to_broadcast(shape),
-                op=MULT,
-            )
+            shape = [P, MIX_HEADS, GROUP_POS, VIEWS]
+            mixw = mixw_pool.tile([P, HEADS, GROUP_POS, VIEWS], F32)
+            for h in range(0, HEADS, MIX_HEADS):
+                nc.gpsimd.tensor_tensor(
+                    out=mixw[:, h : h + MIX_HEADS],
+                    in0=weights_t[:, c, b, h : h + MIX_HEADS, :].unsqueeze(2).to_broadcast(shape),
+                    in1=block_mask[:].unsqueeze(1).to_broadcast(shape),
+                    op=MULT,
+                )
             mix_weights[grp] = mixw
 
         def mix(grp):
@@ -329,52 +396,86 @@ def tile_crossviewattention_pa_kernel(tc, x, scores, Wv, bv, Wo, bo, out):
         def is_group(grp):
             return 0 <= grp < GROUPS
 
-        def is_pass(g):
-            return 0 <= g < PASSES
+        def slab_that_starts_at(grp):
+            slab, offset = divmod(grp, SLAB_GROUPS)
+            return slab if offset == 0 and FIRST_SLAB <= slab < SLABS else None
 
-        wv_start = -(AHEAD_V + AHEAD_X)
-        wo_start = BEHIND_Y - PASSES - 1
+        V, S = nc.vector.tensor_copy, nc.scalar.copy
+        FIRST_IN_LOOP = 1
+        transpose_tokens(0)
+        quantise_tokens(0)
+        regroup_wv(V, 0, 0)
+        regroup_wv(S, 0, 1)
+        softmax_shift(0)
+        regroup_wv(V, 1, 0)
+        regroup_wv(S, 1, 1)
+        softmax_exp(0)
+        quantise_weights("wv", wv_codes, wv_scales, 0, 0)
+        quantise_weights("wv", wv_codes, wv_scales, 1, 0)
+        first_projection(0, 0)
+        softmax_normalise(0)
+        regroup_wv(S, 0, 3)
+        regroup_wv(V, 0, 2)
+        transpose_tokens(1)
+        softmax_transpose(0)
+        regroup_wv(V, 1, 2)
+        regroup_wv(S, 1, 3)
+        quantise_weights("wv", wv_codes, wv_scales, 0, 1)
+        quantise_tokens(1)
+        quantise_weights("wv", wv_codes, wv_scales, 1, 1)
+        first_projection(0, 1)
+        for grp in range(2):
+            build_mix_weights(grp)
+
         for step in range(FIRST_STEP, GROUPS + BEHIND_Y):
             if is_group(step - 1):
                 round_mixed(step - 1)
+            if is_group(step - 2):
+                quantise_mixed(step - 2)
+            part = step - (BEHIND_Y - PASSES * N_HALVES)
+            if 0 < part <= PASSES * N_HALVES:
+                half, g = divmod(part - 1, PASSES)
+                quantise_weights("wo", wo_codes, wo_scales, g, half)
             if is_group(step - BEHIND_Y):
                 second_projection(step - BEHIND_Y)
                 finish(step - BEHIND_Y)
-            if is_group(step - 2):
-                quantise_mixed(step - 2)
-            if is_pass(step - wv_start - 1):
-                quantise_weights("wv", wv_codes, wv_scales, step - wv_start - 1)
-            if is_pass(step - wo_start - 1):
-                quantise_weights("wo", wo_codes, wo_scales, step - wo_start - 1)
-            if is_group(step + AHEAD_V):
-                first_projection(step + AHEAD_V)
+            if FIRST_IN_LOOP <= step + AHEAD_V < GROUPS:
+                for half in range(N_HALVES):
+                    first_projection(step + AHEAD_V, half)
 
             piece = piece_that_starts_at(step + AHEAD_W + 2)
-            if piece is not None:
+            if piece is not None and piece > 0:
                 softmax_exp(piece)
-            if is_pass(step - wv_start):
-                regroup_weights("wv", wv_raw, step - wv_start)
-            if is_pass(step - wo_start):
-                regroup_weights("wo", wo_raw, step - wo_start)
-
-            if is_group(step + AHEAD_V + AHEAD_X):
-                transpose_tokens(step + AHEAD_V + AHEAD_X)
+            slab = slab_that_starts_at(step + AHEAD_V + 4)
+            if slab is not None:
+                order_slab(slab)
+            slab = slab_that_starts_at(step + AHEAD_V + 3)
+            if slab is not None:
+                turn_slab(slab)
+            if TURNED_BY_TENSOR <= step + AHEAD_V + 2 < GROUPS:
+                group_tokens(step + AHEAD_V + 2)
+            elif step + AHEAD_V + 2 < TURNED_BY_TENSOR:
+                transpose_tokens(step + AHEAD_V + 2)
             if is_group(step - 1):
                 transpose_mixed(step - 1)
             piece = piece_that_starts_at(step + AHEAD_W + 1)
             if piece is not None:
                 softmax_transpose(piece)
-            if is_group(step + AHEAD_V + AHEAD_X - 1):
-                quantise_tokens(step + AHEAD_V + AHEAD_X - 1)
+            if is_group(step + AHEAD_V + 1):
+                quantise_tokens(step + AHEAD_V + 1)
+
+            if 0 <= part < PASSES * N_HALVES:
+                half, g = divmod(part, PASSES)
+                regroup_wo(g, half)
 
             piece = piece_that_starts_at(step + AHEAD_W + 2)
-            if piece is not None:
+            if piece is not None and piece > 0:
                 softmax_normalise(piece)
             piece = piece_that_starts_at(step + AHEAD_W + 3)
-            if piece is not None:
+            if piece is not None and piece > 0:
                 softmax_shift(piece)
 
-            if is_group(step + AHEAD_W):
+            if is_group(step + AHEAD_W) and step + AHEAD_W >= 2:
                 build_mix_weights(step + AHEAD_W)
             if is_group(step):
                 mix(step)

@@ -42,8 +42,8 @@ QUAD_FEATURES = K_PASS // QUADS
 AHEAD_V = 1
 AHEAD_W = 2
 BEHIND_Y = 3
+MOST_BEHIND_Y = 4
 FIRST_STEP = -AHEAD_V
-MIX_HEADS = 2
 
 FLOPS = 2 * 2 * SCENES * VIEWS * POSITIONS * FEATURES * FEATURES + 2 * SCENES * VIEWS * VIEWS * POSITIONS * FEATURES
 
@@ -53,12 +53,13 @@ def tile_crossviewattention_pa_kernel(tc, x, scores, Wv, bv, Wo, bo, out):
     with ExitStack() as ctx:
         keep = ctx.enter_context(tc.tile_pool(name="keep", bufs=1))
         x_stage = ctx.enter_context(tc.tile_pool(name="x_stage", bufs=3))
+        slab_stage = ctx.enter_context(tc.tile_pool(name="slab_stage", bufs=2))
         w_stage = ctx.enter_context(tc.tile_pool(name="w_stage", bufs=4))
         s_pool = ctx.enter_context(tc.tile_pool(name="s_pool", bufs=2))
         v_pool = ctx.enter_context(tc.tile_pool(name="v_pool", bufs=AHEAD_V + 2))
         mixw_pool = ctx.enter_context(tc.tile_pool(name="mixw_pool", bufs=AHEAD_W + 2))
-        m_pool = ctx.enter_context(tc.tile_pool(name="m_pool", bufs=BEHIND_Y + 2))
-        y_pool = ctx.enter_context(tc.tile_pool(name="y_pool", bufs=6))
+        m_pool = ctx.enter_context(tc.tile_pool(name="m_pool", bufs=MOST_BEHIND_Y + 1))
+        y_pool = ctx.enter_context(tc.tile_pool(name="y_pool", bufs=8))
         psum = ctx.enter_context(tc.psum_pool(name="psum", bufs=2))
         ctx.enter_context(tc.manual_schedule())
 
@@ -120,25 +121,32 @@ def tile_crossviewattention_pa_kernel(tc, x, scores, Wv, bv, Wo, bo, out):
                 out=score_raw[:, j, :], in_=scores[:, :, j, :, :].rearrange("b i h s -> (b i) h s")
             )
 
+        bias_rows = keep.tile([P, 2, FEATURES], BF16)
+        nc.vector.memset(bias_rows[:], 0.0)
+        ones = keep.tile([P, P], BF16)
+        nc.vector.memset(ones[:], 1.0)
         ident = keep.tile([P, P], F32)
         make_identity(nc, ident[:])
+        warm = keep.tile([P, 1], F32)
+        nc.vector.memset(warm[:], 0.0)
 
         load_tokens(0)
         for j in range(5):
             load_scores(j)
+        nc.scalar.activation(out=warm[:], in_=warm[:], func=EXP)
         for g in range(PASSES):
             load_wv(g, 0)
         for j in range(5, VIEWS):
             load_scores(j)
+        for k, bias in enumerate((bv, bo)):
+            nc.scalar.dma_start(out=bias_rows[0:1, k, :], in_=bias.rearrange("(a n) -> a n", a=1))
         for g in range(PASSES):
             load_wv(g, 1)
         for grp in range(1, TURNED_BY_TENSOR):
             load_tokens(grp)
         load_slab(FIRST_SLAB)
-        nc.sync.dma_start(out=bv_all[:], in_=bv.partition_broadcast(P))
         for g in range(PASSES):
             load_wo(g)
-        nc.sync.dma_start(out=bo_all[:], in_=bo.partition_broadcast(P))
         for slab in range(FIRST_SLAB + 1, SLABS):
             load_slab(slab)
         same_pos = keep.tile([P, GROUP_POS], F32)
@@ -199,7 +207,7 @@ def tile_crossviewattention_pa_kernel(tc, x, scores, Wv, bv, Wo, bo, out):
         turned_slabs = {}
 
         def order_slab(slab):
-            ordered = x_stage.tile([P, VIEWS, PASSES, 2, QUAD], F32, align_bytes=64)
+            ordered = slab_stage.tile([P, VIEWS, PASSES, 2, QUAD], F32, align_bytes=64)
             words = x_slabs[:, slab - FIRST_SLAB].rearrange("p j g k -> p (j g k)").bitcast(F32)
             nc.scalar.copy(
                 out=ordered[:].rearrange("p j g u i -> p (j g) u i"),
@@ -208,7 +216,7 @@ def tile_crossviewattention_pa_kernel(tc, x, scores, Wv, bv, Wo, bo, out):
             ordered_slabs[slab] = ordered
 
         def turn_slab(slab):
-            turned = x_stage.tile([P, VIEWS, PASSES, 2, QUAD], F32, align_bytes=64)
+            turned = slab_stage.tile([P, VIEWS, PASSES, 2, QUAD], F32, align_bytes=64)
             nc.vector.transpose(
                 out=turned[:].rearrange("p j g u r -> p (j g u r)"),
                 in_=ordered_slabs[slab][:].rearrange("p j g u i -> p (j g u i)"),
@@ -243,7 +251,7 @@ def tile_crossviewattention_pa_kernel(tc, x, scores, Wv, bv, Wo, bo, out):
             top = s_pool.tile([P, PIECE_POS], F32)
             nc.vector.tensor_reduce(out=top[:], in_=by_pos, axis=INNERMOST, op=MAX)
             expd = s_pool.tile(piece_shape, F32)
-            nc.gpsimd.tensor_tensor(
+            nc.vector.tensor_tensor(
                 out=expd[:], in0=by_pos, in1=top[:].unsqueeze(2).to_broadcast(piece_shape), op=SUBTRACT
             )
             exponents[piece] = expd
@@ -257,7 +265,7 @@ def tile_crossviewattention_pa_kernel(tc, x, scores, Wv, bv, Wo, bo, out):
             inverse = s_pool.tile([P, PIECE_POS], F32)
             nc.vector.reciprocal(out=inverse[:], in_=total[:])
             weights = s_pool.tile([P, PIECE_CHUNKS, P], F32)
-            nc.gpsimd.tensor_tensor(
+            nc.vector.tensor_tensor(
                 out=weights[:].rearrange("p c (s j) -> p (c s) j", j=VIEWS),
                 in0=exponents[piece][:],
                 in1=inverse[:].unsqueeze(2).to_broadcast(piece_shape),
@@ -278,6 +286,18 @@ def tile_crossviewattention_pa_kernel(tc, x, scores, Wv, bv, Wo, bo, out):
         def piece_that_starts_at(grp):
             piece, offset = divmod(grp, PIECE_GROUPS)
             return piece if offset == 0 and 0 <= piece < PIECES else None
+
+        def spread_bias(k, bias_all):
+            spread = psum.tile([P, FEATURES], BF16, tag="acc_y")
+            for half in range(N_HALVES):
+                nc.tensor.matmul(
+                    out=spread[:, half_cols(half)],
+                    lhsT=ones[:],
+                    rhs=bias_rows[:, k, half_cols(half)],
+                    start=True,
+                    stop=True,
+                )
+            nc.vector.tensor_copy(out=bias_all[:], in_=spread[:])
 
         values = {}
         mix_weights = {}
@@ -305,14 +325,14 @@ def tile_crossviewattention_pa_kernel(tc, x, scores, Wv, bv, Wo, bo, out):
                 )
             nc.scalar.copy(out=values[grp][:, half_cols(half)], in_=acc[:])
 
-        def build_mix_weights(grp):
+        def build_mix_weights(grp, heads):
             c, b = chunk_and_scene(grp)
-            shape = [P, MIX_HEADS, GROUP_POS, VIEWS]
+            shape = [P, heads, GROUP_POS, VIEWS]
             mixw = mixw_pool.tile([P, HEADS, GROUP_POS, VIEWS], F32)
-            for h in range(0, HEADS, MIX_HEADS):
+            for h in range(0, HEADS, heads):
                 nc.gpsimd.tensor_tensor(
-                    out=mixw[:, h : h + MIX_HEADS],
-                    in0=weights_t[:, c, b, h : h + MIX_HEADS, :].unsqueeze(2).to_broadcast(shape),
+                    out=mixw[:, h : h + heads],
+                    in0=weights_t[:, c, b, h : h + heads, :].unsqueeze(2).to_broadcast(shape),
                     in1=block_mask[:].unsqueeze(1).to_broadcast(shape),
                     op=MULT,
                 )
@@ -393,12 +413,20 @@ def tile_crossviewattention_pa_kernel(tc, x, scores, Wv, bv, Wo, bo, out):
                 )
                 nc.sync.dma_start(out=group_rows(out, grp, half_cols(half)), in_=result[:])
 
+        def finish_group(grp):
+            second_projection(grp)
+            finish(grp)
+
         def is_group(grp):
             return 0 <= grp < GROUPS
 
         def slab_that_starts_at(grp):
             slab, offset = divmod(grp, SLAB_GROUPS)
             return slab if offset == 0 and FIRST_SLAB <= slab < SLABS else None
+
+        WO_START = MOST_BEHIND_Y - PASSES * N_HALVES - 1
+        SPREAD_STEPS = {0: (0, bv_all), MOST_BEHIND_Y - 1: (1, bo_all)}
+        FINISH_STEP = [max(grp + BEHIND_Y, MOST_BEHIND_Y + grp // 2) for grp in range(GROUPS)]
 
         V, S = nc.vector.tensor_copy, nc.scalar.copy
         FIRST_IN_LOOP = 1
@@ -409,43 +437,44 @@ def tile_crossviewattention_pa_kernel(tc, x, scores, Wv, bv, Wo, bo, out):
         softmax_shift(0)
         regroup_wv(V, 1, 0)
         regroup_wv(S, 1, 1)
+        regroup_wv(S, 0, 3)
         softmax_exp(0)
         quantise_weights("wv", wv_codes, wv_scales, 0, 0)
         quantise_weights("wv", wv_codes, wv_scales, 1, 0)
-        first_projection(0, 0)
-        softmax_normalise(0)
-        regroup_wv(S, 0, 3)
         regroup_wv(V, 0, 2)
+        softmax_normalise(0)
+        regroup_wv(S, 1, 3)
+        regroup_wv(V, 1, 2)
+        first_projection(0, 0)
         transpose_tokens(1)
         softmax_transpose(0)
-        regroup_wv(V, 1, 2)
-        regroup_wv(S, 1, 3)
         quantise_weights("wv", wv_codes, wv_scales, 0, 1)
-        quantise_tokens(1)
         quantise_weights("wv", wv_codes, wv_scales, 1, 1)
+        quantise_tokens(1)
         first_projection(0, 1)
-        for grp in range(2):
-            build_mix_weights(grp)
+        build_mix_weights(0, 2)
 
-        for step in range(FIRST_STEP, GROUPS + BEHIND_Y):
-            if is_group(step - 1):
-                round_mixed(step - 1)
-            if is_group(step - 2):
-                quantise_mixed(step - 2)
-            part = step - (BEHIND_Y - PASSES * N_HALVES)
-            if 0 < part <= PASSES * N_HALVES:
-                half, g = divmod(part - 1, PASSES)
-                quantise_weights("wo", wo_codes, wo_scales, g, half)
-            if is_group(step - BEHIND_Y):
-                second_projection(step - BEHIND_Y)
-                finish(step - BEHIND_Y)
-            if FIRST_IN_LOOP <= step + AHEAD_V < GROUPS:
-                for half in range(N_HALVES):
-                    first_projection(step + AHEAD_V, half)
-
+        for step in range(FIRST_STEP, GROUPS):
             piece = piece_that_starts_at(step + AHEAD_W + 2)
             if piece is not None and piece > 0:
                 softmax_exp(piece)
+            if is_group(step - 1):
+                round_mixed(step - 1)
+            part = step - WO_START
+            if 1 < part <= PASSES * N_HALVES + 1:
+                half, g = divmod(part - 2, PASSES)
+                quantise_weights("wo", wo_codes, wo_scales, g, half)
+            for grp in range(GROUPS):
+                if FINISH_STEP[grp] == step:
+                    second_projection(grp)
+                    finish(grp)
+            if FIRST_IN_LOOP <= step + AHEAD_V < GROUPS:
+                for half in range(N_HALVES):
+                    first_projection(step + AHEAD_V, half)
+            if is_group(step - 1):
+                transpose_mixed(step - 1)
+            if step + AHEAD_V + 2 < TURNED_BY_TENSOR:
+                transpose_tokens(step + AHEAD_V + 2)
             slab = slab_that_starts_at(step + AHEAD_V + 4)
             if slab is not None:
                 order_slab(slab)
@@ -454,28 +483,36 @@ def tile_crossviewattention_pa_kernel(tc, x, scores, Wv, bv, Wo, bo, out):
                 turn_slab(slab)
             if TURNED_BY_TENSOR <= step + AHEAD_V + 2 < GROUPS:
                 group_tokens(step + AHEAD_V + 2)
-            elif step + AHEAD_V + 2 < TURNED_BY_TENSOR:
-                transpose_tokens(step + AHEAD_V + 2)
-            if is_group(step - 1):
-                transpose_mixed(step - 1)
             piece = piece_that_starts_at(step + AHEAD_W + 1)
             if piece is not None:
                 softmax_transpose(piece)
             if is_group(step + AHEAD_V + 1):
                 quantise_tokens(step + AHEAD_V + 1)
-
             if 0 <= part < PASSES * N_HALVES:
                 half, g = divmod(part, PASSES)
                 regroup_wo(g, half)
-
             piece = piece_that_starts_at(step + AHEAD_W + 2)
             if piece is not None and piece > 0:
                 softmax_normalise(piece)
             piece = piece_that_starts_at(step + AHEAD_W + 3)
             if piece is not None and piece > 0:
                 softmax_shift(piece)
-
-            if is_group(step + AHEAD_W) and step + AHEAD_W >= 2:
-                build_mix_weights(step + AHEAD_W)
+            if is_group(step + AHEAD_W) and step + AHEAD_W >= 1:
+                build_mix_weights(step + AHEAD_W, HEADS)
+            if is_group(step - 1):
+                quantise_mixed(step - 1)
+            if step in SPREAD_STEPS:
+                spread_bias(*SPREAD_STEPS[step])
             if is_group(step):
                 mix(step)
+
+        last = GROUPS - 1
+        round_mixed(last)
+        second_projection(last - 2)
+        transpose_mixed(last)
+        finish(last - 2)
+        second_projection(last - 1)
+        quantise_mixed(last)
+        finish(last - 1)
+        second_projection(last)
+        finish(last)

@@ -39,7 +39,7 @@ QUADS = 4
 QUAD = P // QUADS
 QUAD_FEATURES = K_PASS // QUADS
 
-AHEAD_V = 1
+AHEAD_V = 2
 AHEAD_W = 2
 BEHIND_Y = 3
 MOST_BEHIND_Y = 4
@@ -116,8 +116,8 @@ def tile_crossviewattention_pa_kernel(tc, x, scores, Wv, bv, Wo, bo, out):
                 in_=Wo[g * K_PASS : (g + 1) * K_PASS, :].rearrange("(p t) n -> p t n", t=PACK),
             )
 
-        def load_scores(j):
-            nc.scalar.dma_start(
+        def load_scores(j, queue):
+            queue.dma_start(
                 out=score_raw[:, j, :], in_=scores[:, :, j, :, :].rearrange("b i h s -> (b i) h s")
             )
 
@@ -132,18 +132,18 @@ def tile_crossviewattention_pa_kernel(tc, x, scores, Wv, bv, Wo, bo, out):
 
         load_tokens(0)
         for j in range(5):
-            load_scores(j)
+            load_scores(j, nc.scalar)
         nc.scalar.activation(out=warm[:], in_=warm[:], func=EXP)
         for g in range(PASSES):
             load_wv(g, 0)
         for j in range(5, VIEWS):
-            load_scores(j)
-        for k, bias in enumerate((bv, bo)):
-            nc.scalar.dma_start(out=bias_rows[0:1, k, :], in_=bias.rearrange("(a n) -> a n", a=1))
+            load_scores(j, nc.sync)
         for g in range(PASSES):
             load_wv(g, 1)
         for grp in range(1, TURNED_BY_TENSOR):
             load_tokens(grp)
+        for k, bias in enumerate((bv, bo)):
+            nc.sync.dma_start(out=bias_rows[0:1, k, :], in_=bias.rearrange("(a n) -> a n", a=1))
         load_slab(FIRST_SLAB)
         for g in range(PASSES):
             load_wo(g)
@@ -431,8 +431,8 @@ def tile_crossviewattention_pa_kernel(tc, x, scores, Wv, bv, Wo, bo, out):
         V, S = nc.vector.tensor_copy, nc.scalar.copy
         FIRST_IN_LOOP = 1
         transpose_tokens(0)
-        quantise_tokens(0)
         regroup_wv(V, 0, 0)
+        quantise_tokens(0)
         regroup_wv(S, 0, 1)
         softmax_shift(0)
         regroup_wv(V, 1, 0)
@@ -450,7 +450,6 @@ def tile_crossviewattention_pa_kernel(tc, x, scores, Wv, bv, Wo, bo, out):
         softmax_transpose(0)
         quantise_weights("wv", wv_codes, wv_scales, 0, 1)
         quantise_weights("wv", wv_codes, wv_scales, 1, 1)
-        quantise_tokens(1)
         first_projection(0, 1)
         build_mix_weights(0, 2)
 
@@ -460,6 +459,8 @@ def tile_crossviewattention_pa_kernel(tc, x, scores, Wv, bv, Wo, bo, out):
                 softmax_exp(piece)
             if is_group(step - 1):
                 round_mixed(step - 1)
+            if is_group(step - 2):
+                quantise_mixed(step - 2)
             part = step - WO_START
             if 1 < part <= PASSES * N_HALVES + 1:
                 half, g = divmod(part - 2, PASSES)
@@ -468,13 +469,10 @@ def tile_crossviewattention_pa_kernel(tc, x, scores, Wv, bv, Wo, bo, out):
                 if FINISH_STEP[grp] == step:
                     second_projection(grp)
                     finish(grp)
-            if FIRST_IN_LOOP <= step + AHEAD_V < GROUPS:
-                for half in range(N_HALVES):
-                    first_projection(step + AHEAD_V, half)
-            if is_group(step - 1):
-                transpose_mixed(step - 1)
             if step + AHEAD_V + 2 < TURNED_BY_TENSOR:
                 transpose_tokens(step + AHEAD_V + 2)
+            if is_group(step - 1):
+                transpose_mixed(step - 1)
             slab = slab_that_starts_at(step + AHEAD_V + 4)
             if slab is not None:
                 order_slab(slab)
@@ -499,15 +497,17 @@ def tile_crossviewattention_pa_kernel(tc, x, scores, Wv, bv, Wo, bo, out):
                 softmax_shift(piece)
             if is_group(step + AHEAD_W) and step + AHEAD_W >= 1:
                 build_mix_weights(step + AHEAD_W, HEADS)
-            if is_group(step - 1):
-                quantise_mixed(step - 1)
             if step in SPREAD_STEPS:
                 spread_bias(*SPREAD_STEPS[step])
             if is_group(step):
                 mix(step)
+            if FIRST_IN_LOOP <= step + AHEAD_V < GROUPS:
+                for half in range(N_HALVES):
+                    first_projection(step + AHEAD_V, half)
 
         last = GROUPS - 1
         round_mixed(last)
+        quantise_mixed(last - 1)
         second_projection(last - 2)
         transpose_mixed(last)
         finish(last - 2)

@@ -13,6 +13,7 @@ SUBTRACT = mybir.AluOpType.subtract
 MULT = mybir.AluOpType.mult
 MAX = mybir.AluOpType.max
 INNERMOST = mybir.AxisListType.X
+COPY = mybir.ActivationFunctionType.Copy
 EXP = mybir.ActivationFunctionType.Exp
 
 P = 128
@@ -33,16 +34,17 @@ PIECE_POS = PIECE_CHUNKS * GROUP_POS
 PIECES = CHUNKS // PIECE_CHUNKS
 SLAB_GROUPS = 2
 SLABS = GROUPS // SLAB_GROUPS
-TURNED_BY_TENSOR = 4
+TURNED_BY_TENSOR = 8
 FIRST_SLAB = TURNED_BY_TENSOR // SLAB_GROUPS
 QUADS = 4
 QUAD = P // QUADS
 QUAD_FEATURES = K_PASS // QUADS
 
 AHEAD_V = 2
+LEAD = 4
 AHEAD_W = 2
 BEHIND_Y = 3
-MOST_BEHIND_Y = 4
+MOST_BEHIND_Y = 5
 FIRST_STEP = -AHEAD_V
 
 FLOPS = 2 * 2 * SCENES * VIEWS * POSITIONS * FEATURES * FEATURES + 2 * SCENES * VIEWS * VIEWS * POSITIONS * FEATURES
@@ -57,9 +59,9 @@ def tile_crossviewattention_pa_kernel(tc, x, scores, Wv, bv, Wo, bo, out):
         w_stage = ctx.enter_context(tc.tile_pool(name="w_stage", bufs=4))
         s_pool = ctx.enter_context(tc.tile_pool(name="s_pool", bufs=2))
         v_pool = ctx.enter_context(tc.tile_pool(name="v_pool", bufs=AHEAD_V + 2))
-        mixw_pool = ctx.enter_context(tc.tile_pool(name="mixw_pool", bufs=AHEAD_W + 2))
+        big = ctx.enter_context(tc.tile_pool(name="big", bufs=3))
         m_pool = ctx.enter_context(tc.tile_pool(name="m_pool", bufs=MOST_BEHIND_Y + 1))
-        y_pool = ctx.enter_context(tc.tile_pool(name="y_pool", bufs=8))
+        y_pool = ctx.enter_context(tc.tile_pool(name="y_pool", bufs=6))
         psum = ctx.enter_context(tc.psum_pool(name="psum", bufs=2))
         ctx.enter_context(tc.manual_schedule())
 
@@ -80,10 +82,10 @@ def tile_crossviewattention_pa_kernel(tc, x, scores, Wv, bv, Wo, bo, out):
         x_slabs = keep.tile([P, SLABS - FIRST_SLAB, VIEWS, PASSES, QUAD_FEATURES], BF16)
         x_codes = keep.tile([P, GROUPS, PASSES * P], U32, align_bytes=64)
         x_scales = keep.tile([P, GROUPS, PASSES * P], U8, align_bytes=64)
-        wv_raw = keep.tile([P, PASSES, PACK, FEATURES], BF16)
+        wv_raw = big.tile([P, PASSES, PACK, FEATURES], BF16, tag="big")
         wv_codes = keep.tile([P, PASSES, FEATURES], U32, align_bytes=64)
         wv_scales = keep.tile([P, PASSES, FEATURES], U8, align_bytes=64)
-        wo_raw = keep.tile([P, PASSES, PACK, FEATURES], BF16)
+        wo_raw = big.tile([P, PASSES, PACK, FEATURES], BF16, tag="big")
         wo_codes = keep.tile([P, PASSES, FEATURES], U32, align_bytes=64)
         wo_scales = keep.tile([P, PASSES, FEATURES], U8, align_bytes=64)
         score_raw = keep.tile([P, VIEWS, POSITIONS], BF16)
@@ -130,24 +132,25 @@ def tile_crossviewattention_pa_kernel(tc, x, scores, Wv, bv, Wo, bo, out):
         warm = keep.tile([P, 1], F32)
         nc.vector.memset(warm[:], 0.0)
 
-        load_tokens(0)
-        for j in range(5):
+        nc.gpsimd.dma_start(out=bias_rows[0:1, 0, :], in_=bv.rearrange("(a n) -> a n", a=1))
+        for j in range(7):
             load_scores(j, nc.scalar)
+            if j == 1:
+                load_tokens(0)
+                for g in range(PASSES):
+                    load_wv(g, 0)
+        load_scores(7, nc.gpsimd)
+        nc.gpsimd.dma_start(out=bias_rows[0:1, 1, :], in_=bo.rearrange("(a n) -> a n", a=1))
         nc.scalar.activation(out=warm[:], in_=warm[:], func=EXP)
         for g in range(PASSES):
-            load_wv(g, 0)
-        for j in range(5, VIEWS):
-            load_scores(j, nc.sync)
-        for g in range(PASSES):
             load_wv(g, 1)
-        for grp in range(1, TURNED_BY_TENSOR):
+        for grp in range(1, 4):
             load_tokens(grp)
-        for k, bias in enumerate((bv, bo)):
-            nc.sync.dma_start(out=bias_rows[0:1, k, :], in_=bias.rearrange("(a n) -> a n", a=1))
-        load_slab(FIRST_SLAB)
         for g in range(PASSES):
             load_wo(g)
-        for slab in range(FIRST_SLAB + 1, SLABS):
+        for grp in range(4, TURNED_BY_TENSOR):
+            load_tokens(grp)
+        for slab in range(FIRST_SLAB, SLABS):
             load_slab(slab)
         same_pos = keep.tile([P, GROUP_POS], F32)
         nc.vector.tensor_reduce(
@@ -325,20 +328,39 @@ def tile_crossviewattention_pa_kernel(tc, x, scores, Wv, bv, Wo, bo, out):
                 )
             nc.scalar.copy(out=values[grp][:, half_cols(half)], in_=acc[:])
 
+        def open_mix_weights(piece):
+            piece_mixw = big.tile([P, PIECE_GROUPS, HEADS, GROUP_POS, VIEWS], F32, tag="big")
+            mix_weights[piece] = piece_mixw
+
+        def group_in_piece(grp):
+            c, b = chunk_and_scene(grp)
+            piece, part = divmod(c, PIECE_CHUNKS)
+            return piece, part * SCENES + b
+
         def build_mix_weights(grp, heads):
+            piece, part = group_in_piece(grp)
             c, b = chunk_and_scene(grp)
             shape = [P, heads, GROUP_POS, VIEWS]
-            mixw = mixw_pool.tile([P, HEADS, GROUP_POS, VIEWS], F32)
             for h in range(0, HEADS, heads):
                 nc.gpsimd.tensor_tensor(
-                    out=mixw[:, h : h + heads],
+                    out=mix_weights[piece][:, part, h : h + heads],
                     in0=weights_t[:, c, b, h : h + heads, :].unsqueeze(2).to_broadcast(shape),
                     in1=block_mask[:].unsqueeze(1).to_broadcast(shape),
                     op=MULT,
                 )
-            mix_weights[grp] = mixw
+
+        def spread_mix_weights(piece, positions):
+            chunks = slice(piece * PIECE_CHUNKS, (piece + 1) * PIECE_CHUNKS)
+            for s in positions:
+                nc.scalar.activation(
+                    out=mix_weights[piece][:, :, :, s, :],
+                    in_=weights_t[:, chunks].rearrange("p c b h i -> p (c b) h i"),
+                    func=COPY,
+                    scale=same_pos[:, s : s + 1],
+                )
 
         def mix(grp):
+            piece, part = group_in_piece(grp)
             sums = []
             for g in range(PASSES):
                 acc = psum.tile([P, PACK, P], F32, tag="acc_mix")
@@ -346,7 +368,7 @@ def tile_crossviewattention_pa_kernel(tc, x, scores, Wv, bv, Wo, bo, out):
                     h = g * PACK + t
                     nc.tensor.matmul(
                         out=acc[:, t, :],
-                        lhsT=mix_weights[grp][:, h, :, :].rearrange("p s i -> p (s i)"),
+                        lhsT=mix_weights[piece][:, part, h, :, :].rearrange("p s i -> p (s i)"),
                         rhs=values[grp][:, h * P : (h + 1) * P],
                         start=True,
                         stop=True,
@@ -425,36 +447,38 @@ def tile_crossviewattention_pa_kernel(tc, x, scores, Wv, bv, Wo, bo, out):
             return slab if offset == 0 and FIRST_SLAB <= slab < SLABS else None
 
         WO_START = MOST_BEHIND_Y - PASSES * N_HALVES - 1
-        SPREAD_STEPS = {0: (0, bv_all), MOST_BEHIND_Y - 1: (1, bo_all)}
+        SPREAD_STEPS = {MOST_BEHIND_Y - 1: (1, bo_all)}
         FINISH_STEP = [max(grp + BEHIND_Y, MOST_BEHIND_Y + grp // 2) for grp in range(GROUPS)]
 
         V, S = nc.vector.tensor_copy, nc.scalar.copy
         FIRST_IN_LOOP = 1
+        spread_bias(0, bv_all)
         transpose_tokens(0)
         regroup_wv(V, 0, 0)
         quantise_tokens(0)
         regroup_wv(S, 0, 1)
-        softmax_shift(0)
         regroup_wv(V, 1, 0)
         regroup_wv(S, 1, 1)
-        regroup_wv(S, 0, 3)
-        softmax_exp(0)
         quantise_weights("wv", wv_codes, wv_scales, 0, 0)
         quantise_weights("wv", wv_codes, wv_scales, 1, 0)
+        softmax_shift(0)
+        regroup_wv(S, 0, 3)
+        softmax_exp(0)
         regroup_wv(V, 0, 2)
-        softmax_normalise(0)
+        first_projection(0, 0)
         regroup_wv(S, 1, 3)
         regroup_wv(V, 1, 2)
-        first_projection(0, 0)
-        transpose_tokens(1)
-        softmax_transpose(0)
+        softmax_normalise(0)
         quantise_weights("wv", wv_codes, wv_scales, 0, 1)
         quantise_weights("wv", wv_codes, wv_scales, 1, 1)
+        transpose_tokens(1)
+        softmax_transpose(0)
         first_projection(0, 1)
+        open_mix_weights(0)
         build_mix_weights(0, 2)
 
         for step in range(FIRST_STEP, GROUPS):
-            piece = piece_that_starts_at(step + AHEAD_W + 2)
+            piece = piece_that_starts_at(step + LEAD + 1)
             if piece is not None and piece > 0:
                 softmax_exp(piece)
             if is_group(step - 1):
@@ -481,22 +505,24 @@ def tile_crossviewattention_pa_kernel(tc, x, scores, Wv, bv, Wo, bo, out):
                 turn_slab(slab)
             if TURNED_BY_TENSOR <= step + AHEAD_V + 2 < GROUPS:
                 group_tokens(step + AHEAD_V + 2)
-            piece = piece_that_starts_at(step + AHEAD_W + 1)
-            if piece is not None:
-                softmax_transpose(piece)
             if is_group(step + AHEAD_V + 1):
                 quantise_tokens(step + AHEAD_V + 1)
             if 0 <= part < PASSES * N_HALVES:
                 half, g = divmod(part, PASSES)
                 regroup_wo(g, half)
-            piece = piece_that_starts_at(step + AHEAD_W + 2)
+            piece = piece_that_starts_at(step + LEAD + 1)
             if piece is not None and piece > 0:
                 softmax_normalise(piece)
-            piece = piece_that_starts_at(step + AHEAD_W + 3)
+            piece = piece_that_starts_at(step + LEAD + 2)
             if piece is not None and piece > 0:
                 softmax_shift(piece)
-            if is_group(step + AHEAD_W) and step + AHEAD_W >= 1:
-                build_mix_weights(step + AHEAD_W, HEADS)
+            if 1 <= step + AHEAD_W < PIECE_GROUPS:
+                build_mix_weights(step + AHEAD_W, 2)
+            piece, quarter = divmod(step + PIECE_GROUPS, PIECE_GROUPS)
+            if 0 < piece < PIECES and quarter > 0:
+                if quarter == 1:
+                    open_mix_weights(piece)
+                spread_mix_weights(piece, range(quarter * 6 - 6, min(quarter * 6, GROUP_POS)))
             if step in SPREAD_STEPS:
                 spread_bias(*SPREAD_STEPS[step])
             if is_group(step):
@@ -504,6 +530,10 @@ def tile_crossviewattention_pa_kernel(tc, x, scores, Wv, bv, Wo, bo, out):
             if FIRST_IN_LOOP <= step + AHEAD_V < GROUPS:
                 for half in range(N_HALVES):
                     first_projection(step + AHEAD_V, half)
+
+            piece = piece_that_starts_at(step + LEAD)
+            if piece is not None:
+                softmax_transpose(piece)
 
         last = GROUPS - 1
         round_mixed(last)

@@ -42,9 +42,10 @@ QUAD_FEATURES = K_PASS // QUADS
 
 AHEAD_V = 2
 LEAD = 4
+BY_GPSIMD = 8
 AHEAD_W = 2
 BEHIND_Y = 3
-MOST_BEHIND_Y = 5
+MOST_BEHIND_Y = 4
 FIRST_STEP = -AHEAD_V
 
 FLOPS = 2 * 2 * SCENES * VIEWS * POSITIONS * FEATURES * FEATURES + 2 * SCENES * VIEWS * VIEWS * POSITIONS * FEATURES
@@ -124,7 +125,7 @@ def tile_crossviewattention_pa_kernel(tc, x, scores, Wv, bv, Wo, bo, out):
             )
 
         bias_rows = keep.tile([P, 2, FEATURES], BF16)
-        nc.vector.memset(bias_rows[:], 0.0)
+        nc.vector.memset(bias_rows[:].rearrange("p k n -> p (k n)").bitcast(U32), 0)
         ones = keep.tile([P, P], BF16)
         nc.vector.memset(ones[:], 1.0)
         ident = keep.tile([P, P], F32)
@@ -290,7 +291,9 @@ def tile_crossviewattention_pa_kernel(tc, x, scores, Wv, bv, Wo, bo, out):
             piece, offset = divmod(grp, PIECE_GROUPS)
             return piece if offset == 0 and 0 <= piece < PIECES else None
 
-        def spread_bias(k, bias_all):
+        spread_sums = {}
+
+        def spread_bias(k):
             spread = psum.tile([P, FEATURES], BF16, tag="acc_y")
             for half in range(N_HALVES):
                 nc.tensor.matmul(
@@ -300,7 +303,10 @@ def tile_crossviewattention_pa_kernel(tc, x, scores, Wv, bv, Wo, bo, out):
                     start=True,
                     stop=True,
                 )
-            nc.vector.tensor_copy(out=bias_all[:], in_=spread[:])
+            spread_sums[k] = spread
+
+        def store_bias(k, bias_all):
+            nc.vector.tensor_copy(out=bias_all[:], in_=spread_sums[k][:])
 
         values = {}
         mix_weights = {}
@@ -412,7 +418,7 @@ def tile_crossviewattention_pa_kernel(tc, x, scores, Wv, bv, Wo, bo, out):
             m_codes, m_scales = mixed_codes[grp]
             sums = []
             for half in range(N_HALVES):
-                acc = psum.tile([P, N_TILE], F32, tag="acc_y")
+                acc = psum.tile([P, N_TILE], F32, tag="acc_v" if grp == GROUPS - 2 else "acc_y")
                 for g in range(PASSES):
                     toks = slice(g * P, (g + 1) * P)
                     nc.tensor.matmul_mx(
@@ -433,7 +439,8 @@ def tile_crossviewattention_pa_kernel(tc, x, scores, Wv, bv, Wo, bo, out):
                 nc.vector.tensor_tensor(
                     out=result[:], in0=out_sums[grp][half][:], in1=bo_all[:, half_cols(half)], op=ADD
                 )
-                nc.sync.dma_start(out=group_rows(out, grp, half_cols(half)), in_=result[:])
+                queue = nc.scalar if grp == GROUPS - 1 and half == 1 else nc.sync
+                queue.dma_start(out=group_rows(out, grp, half_cols(half)), in_=result[:])
 
         def finish_group(grp):
             second_projection(grp)
@@ -446,13 +453,12 @@ def tile_crossviewattention_pa_kernel(tc, x, scores, Wv, bv, Wo, bo, out):
             slab, offset = divmod(grp, SLAB_GROUPS)
             return slab if offset == 0 and FIRST_SLAB <= slab < SLABS else None
 
-        WO_START = MOST_BEHIND_Y - PASSES * N_HALVES - 1
-        SPREAD_STEPS = {MOST_BEHIND_Y - 1: (1, bo_all)}
+        WO_START = -2
+        SPREAD_BO_STEP = MOST_BEHIND_Y - 1
         FINISH_STEP = [max(grp + BEHIND_Y, MOST_BEHIND_Y + grp // 2) for grp in range(GROUPS)]
 
         V, S = nc.vector.tensor_copy, nc.scalar.copy
         FIRST_IN_LOOP = 1
-        spread_bias(0, bv_all)
         transpose_tokens(0)
         regroup_wv(V, 0, 0)
         quantise_tokens(0)
@@ -474,6 +480,7 @@ def tile_crossviewattention_pa_kernel(tc, x, scores, Wv, bv, Wo, bo, out):
         transpose_tokens(1)
         softmax_transpose(0)
         first_projection(0, 1)
+        spread_bias(0)
         open_mix_weights(0)
         build_mix_weights(0, 2)
 
@@ -493,6 +500,9 @@ def tile_crossviewattention_pa_kernel(tc, x, scores, Wv, bv, Wo, bo, out):
                 if FINISH_STEP[grp] == step:
                     second_projection(grp)
                     finish(grp)
+            piece = piece_that_starts_at(step + LEAD)
+            if piece is not None:
+                softmax_normalise(piece)
             if step + AHEAD_V + 2 < TURNED_BY_TENSOR:
                 transpose_tokens(step + AHEAD_V + 2)
             if is_group(step - 1):
@@ -507,24 +517,23 @@ def tile_crossviewattention_pa_kernel(tc, x, scores, Wv, bv, Wo, bo, out):
                 group_tokens(step + AHEAD_V + 2)
             if is_group(step + AHEAD_V + 1):
                 quantise_tokens(step + AHEAD_V + 1)
-            if 0 <= part < PASSES * N_HALVES:
-                half, g = divmod(part, PASSES)
-                regroup_wo(g, half)
-            piece = piece_that_starts_at(step + LEAD + 1)
-            if piece is not None and piece > 0:
-                softmax_normalise(piece)
             piece = piece_that_starts_at(step + LEAD + 2)
             if piece is not None and piece > 0:
                 softmax_shift(piece)
-            if 1 <= step + AHEAD_W < PIECE_GROUPS:
+            if 1 <= step + AHEAD_W < BY_GPSIMD:
+                if (step + AHEAD_W) % PIECE_GROUPS == 0:
+                    open_mix_weights((step + AHEAD_W) // PIECE_GROUPS)
                 build_mix_weights(step + AHEAD_W, 2)
             piece, quarter = divmod(step + PIECE_GROUPS, PIECE_GROUPS)
-            if 0 < piece < PIECES and quarter > 0:
+            if BY_GPSIMD <= piece * PIECE_GROUPS < GROUPS and quarter > 0:
                 if quarter == 1:
                     open_mix_weights(piece)
                 spread_mix_weights(piece, range(quarter * 6 - 6, min(quarter * 6, GROUP_POS)))
-            if step in SPREAD_STEPS:
-                spread_bias(*SPREAD_STEPS[step])
+            if step == SPREAD_BO_STEP:
+                spread_bias(1)
+                store_bias(1, bo_all)
+            if step == 0:
+                store_bias(0, bv_all)
             if is_group(step):
                 mix(step)
             if FIRST_IN_LOOP <= step + AHEAD_V < GROUPS:
@@ -534,6 +543,9 @@ def tile_crossviewattention_pa_kernel(tc, x, scores, Wv, bv, Wo, bo, out):
             piece = piece_that_starts_at(step + LEAD)
             if piece is not None:
                 softmax_transpose(piece)
+            if 0 <= part < PASSES * N_HALVES:
+                half, g = divmod(part, PASSES)
+                regroup_wo(g, half)
 
         last = GROUPS - 1
         round_mixed(last)

@@ -42,7 +42,7 @@ QUAD_FEATURES = K_PASS // QUADS
 
 AHEAD_V = 2
 LEAD = 4
-BY_GPSIMD = 8
+BY_GPSIMD = 4
 AHEAD_W = 2
 BEHIND_Y = 3
 MOST_BEHIND_Y = 4
@@ -55,6 +55,7 @@ def tile_crossviewattention_pa_kernel(tc, x, scores, Wv, bv, Wo, bo, out):
     nc = tc.nc
     with ExitStack() as ctx:
         keep = ctx.enter_context(tc.tile_pool(name="keep", bufs=1))
+        x_pool = ctx.enter_context(tc.tile_pool(name="x_pool", bufs=5))
         x_stage = ctx.enter_context(tc.tile_pool(name="x_stage", bufs=3))
         slab_stage = ctx.enter_context(tc.tile_pool(name="slab_stage", bufs=2))
         w_stage = ctx.enter_context(tc.tile_pool(name="w_stage", bufs=4))
@@ -81,8 +82,6 @@ def tile_crossviewattention_pa_kernel(tc, x, scores, Wv, bv, Wo, bo, out):
 
         x_rows = keep.tile([P, TURNED_BY_TENSOR, FEATURES], BF16)
         x_slabs = keep.tile([P, SLABS - FIRST_SLAB, VIEWS, PASSES, QUAD_FEATURES], BF16)
-        x_codes = keep.tile([P, GROUPS, PASSES * P], U32, align_bytes=64)
-        x_scales = keep.tile([P, GROUPS, PASSES * P], U8, align_bytes=64)
         wv_raw = big.tile([P, PASSES, PACK, FEATURES], BF16, tag="big")
         wv_codes = keep.tile([P, PASSES, FEATURES], U32, align_bytes=64)
         wv_scales = keep.tile([P, PASSES, FEATURES], U8, align_bytes=64)
@@ -192,6 +191,7 @@ def tile_crossviewattention_pa_kernel(tc, x, scores, Wv, bv, Wo, bo, out):
             regroup_weights(nc.scalar.copy, "wo", wo_raw, g, 2 * half + 1)
 
         grouped_tokens = {}
+        token_codes = {}
 
         def transpose_tokens(grp):
             words = x_rows[:, grp, :].bitcast(F32)
@@ -239,9 +239,12 @@ def tile_crossviewattention_pa_kernel(tc, x, scores, Wv, bv, Wo, bo, out):
             grouped_tokens[grp] = grouped_x
 
         def quantise_tokens(grp):
+            x_codes = x_pool.tile([P, PASSES * P], U32, align_bytes=64)
+            x_scales = x_pool.tile([P, PASSES * P], U8, align_bytes=64)
+            token_codes[grp] = (x_codes, x_scales)
             nc.vector.quantize_mx(
-                out=x_codes[:, grp, :].bitcast(FP8X4),
-                scales=x_scales[:, grp, :],
+                out=x_codes[:].bitcast(FP8X4),
+                scales=x_scales[:],
                 in_=grouped_tokens[grp][:].rearrange("p g n t -> p (g n t)"),
             )
 
@@ -320,13 +323,14 @@ def tile_crossviewattention_pa_kernel(tc, x, scores, Wv, bv, Wo, bo, out):
             if half == 0:
                 v_rows = v_pool.tile([P, FEATURES], F32)
                 values[grp] = v_rows
+            x_codes, x_scales = token_codes[grp]
             acc = psum.tile([P, N_TILE], F32, tag="acc_v")
             for g in range(PASSES):
                 toks = slice(g * P, (g + 1) * P)
                 nc.tensor.matmul_mx(
                     out=acc[:],
-                    lhsT=x_codes[:, grp, toks].bitcast(FP8X4),
-                    lhsT_scale=x_scales[:, grp, toks],
+                    lhsT=x_codes[:, toks].bitcast(FP8X4),
+                    lhsT_scale=x_scales[:, toks],
                     rhs=wv_codes[:, g, half_cols(half)].bitcast(FP8X4),
                     rhs_scale=wv_scales[:, g, half_cols(half)],
                     start=(g == 0),
@@ -348,7 +352,7 @@ def tile_crossviewattention_pa_kernel(tc, x, scores, Wv, bv, Wo, bo, out):
             c, b = chunk_and_scene(grp)
             shape = [P, heads, GROUP_POS, VIEWS]
             for h in range(0, HEADS, heads):
-                nc.gpsimd.tensor_tensor(
+                nc.vector.tensor_tensor(
                     out=mix_weights[piece][:, part, h : h + heads],
                     in0=weights_t[:, c, b, h : h + heads, :].unsqueeze(2).to_broadcast(shape),
                     in1=block_mask[:].unsqueeze(1).to_broadcast(shape),
@@ -482,7 +486,7 @@ def tile_crossviewattention_pa_kernel(tc, x, scores, Wv, bv, Wo, bo, out):
         first_projection(0, 1)
         spread_bias(0)
         open_mix_weights(0)
-        build_mix_weights(0, 2)
+        build_mix_weights(0, HEADS // 2)
 
         for step in range(FIRST_STEP, GROUPS):
             piece = piece_that_starts_at(step + LEAD + 1)
@@ -523,7 +527,7 @@ def tile_crossviewattention_pa_kernel(tc, x, scores, Wv, bv, Wo, bo, out):
             if 1 <= step + AHEAD_W < BY_GPSIMD:
                 if (step + AHEAD_W) % PIECE_GROUPS == 0:
                     open_mix_weights((step + AHEAD_W) // PIECE_GROUPS)
-                build_mix_weights(step + AHEAD_W, 2)
+                build_mix_weights(step + AHEAD_W, HEADS)
             piece, quarter = divmod(step + PIECE_GROUPS, PIECE_GROUPS)
             if BY_GPSIMD <= piece * PIECE_GROUPS < GROUPS and quarter > 0:
                 if quarter == 1:

@@ -32,21 +32,24 @@ PIECE_CHUNKS = 2
 PIECE_GROUPS = PIECE_CHUNKS * SCENES
 PIECE_POS = PIECE_CHUNKS * GROUP_POS
 PIECES = CHUNKS // PIECE_CHUNKS
+
+TURNED_BY_TENSOR = 8
 SLAB_GROUPS = 2
 SLABS = GROUPS // SLAB_GROUPS
-TURNED_BY_TENSOR = 8
 FIRST_SLAB = TURNED_BY_TENSOR // SLAB_GROUPS
 QUADS = 4
 QUAD = P // QUADS
 QUAD_FEATURES = K_PASS // QUADS
 
 AHEAD_V = 2
-LEAD = 4
-BY_GPSIMD = 4
-AHEAD_W = 2
+AHEAD_X = AHEAD_V + 2
 BEHIND_Y = 3
-MOST_BEHIND_Y = 4
+FIRST_FINISH = 4
+WO_LEAD = 6
 FIRST_STEP = -AHEAD_V
+EARLY_GROUPS = 3
+PAIRED = range(6, 14)
+SCALAR_LOADS = 7
 
 FLOPS = 2 * 2 * SCENES * VIEWS * POSITIONS * FEATURES * FEATURES + 2 * SCENES * VIEWS * VIEWS * POSITIONS * FEATURES
 
@@ -62,7 +65,7 @@ def tile_crossviewattention_pa_kernel(tc, x, scores, Wv, bv, Wo, bo, out):
         s_pool = ctx.enter_context(tc.tile_pool(name="s_pool", bufs=2))
         v_pool = ctx.enter_context(tc.tile_pool(name="v_pool", bufs=AHEAD_V + 2))
         big = ctx.enter_context(tc.tile_pool(name="big", bufs=3))
-        m_pool = ctx.enter_context(tc.tile_pool(name="m_pool", bufs=MOST_BEHIND_Y + 1))
+        m_pool = ctx.enter_context(tc.tile_pool(name="m_pool", bufs=5))
         y_pool = ctx.enter_context(tc.tile_pool(name="y_pool", bufs=6))
         psum = ctx.enter_context(tc.psum_pool(name="psum", bufs=2))
         ctx.enter_context(tc.manual_schedule())
@@ -123,8 +126,8 @@ def tile_crossviewattention_pa_kernel(tc, x, scores, Wv, bv, Wo, bo, out):
                 out=score_raw[:, j, :], in_=scores[:, :, j, :, :].rearrange("b i h s -> (b i) h s")
             )
 
-        bias_rows = keep.tile([P, 2, FEATURES], BF16)
-        nc.vector.memset(bias_rows[:].rearrange("p k n -> p (k n)").bitcast(U32), 0)
+        bias_rows = keep.tile([P, FEATURES], BF16)
+        nc.vector.memset(bias_rows[:].bitcast(U32), 0)
         ones = keep.tile([P, P], BF16)
         nc.vector.memset(ones[:], 1.0)
         ident = keep.tile([P, P], F32)
@@ -132,15 +135,15 @@ def tile_crossviewattention_pa_kernel(tc, x, scores, Wv, bv, Wo, bo, out):
         warm = keep.tile([P, 1], F32)
         nc.vector.memset(warm[:], 0.0)
 
-        nc.gpsimd.dma_start(out=bias_rows[0:1, 0, :], in_=bv.rearrange("(a n) -> a n", a=1))
-        for j in range(7):
+        nc.gpsimd.dma_start(out=bias_rows[0:1, :], in_=bv.rearrange("(a n) -> a n", a=1))
+        for j in range(SCALAR_LOADS):
             load_scores(j, nc.scalar)
             if j == 1:
                 load_tokens(0)
                 for g in range(PASSES):
                     load_wv(g, 0)
-        load_scores(7, nc.gpsimd)
-        nc.gpsimd.dma_start(out=bias_rows[0:1, 1, :], in_=bo.rearrange("(a n) -> a n", a=1))
+        for j in range(SCALAR_LOADS, VIEWS):
+            load_scores(j, nc.gpsimd)
         nc.scalar.activation(out=warm[:], in_=warm[:], func=EXP)
         for g in range(PASSES):
             load_wv(g, 1)
@@ -152,13 +155,10 @@ def tile_crossviewattention_pa_kernel(tc, x, scores, Wv, bv, Wo, bo, out):
             load_tokens(grp)
         for slab in range(FIRST_SLAB, SLABS):
             load_slab(slab)
+        nc.sync.dma_start(out=bo_all[:], in_=bo.partition_broadcast(P))
         same_pos = keep.tile([P, GROUP_POS], F32)
         nc.vector.tensor_reduce(
             out=same_pos[:], in_=ident[:].rearrange("p (s i) -> p s i", i=VIEWS), axis=INNERMOST, op=ADD
-        )
-        block_mask = keep.tile([P, GROUP_POS, VIEWS], F32)
-        nc.vector.tensor_copy(
-            out=block_mask[:], in_=same_pos[:].unsqueeze(2).to_broadcast([P, GROUP_POS, VIEWS])
         )
 
         grouped_weights = {}
@@ -292,24 +292,24 @@ def tile_crossviewattention_pa_kernel(tc, x, scores, Wv, bv, Wo, bo, out):
 
         def piece_that_starts_at(grp):
             piece, offset = divmod(grp, PIECE_GROUPS)
-            return piece if offset == 0 and 0 <= piece < PIECES else None
+            return piece if offset == 0 and 0 < piece < PIECES else None
 
-        spread_sums = {}
+        spread_sums = []
 
-        def spread_bias(k):
+        def spread_bias():
             spread = psum.tile([P, FEATURES], BF16, tag="acc_y")
             for half in range(N_HALVES):
                 nc.tensor.matmul(
                     out=spread[:, half_cols(half)],
                     lhsT=ones[:],
-                    rhs=bias_rows[:, k, half_cols(half)],
+                    rhs=bias_rows[:, half_cols(half)],
                     start=True,
                     stop=True,
                 )
-            spread_sums[k] = spread
+            spread_sums.append(spread)
 
-        def store_bias(k, bias_all):
-            nc.vector.tensor_copy(out=bias_all[:], in_=spread_sums[k][:])
+        def store_bias():
+            nc.vector.tensor_copy(out=bv_all[:], in_=spread_sums[0][:])
 
         values = {}
         mix_weights = {}
@@ -342,35 +342,21 @@ def tile_crossviewattention_pa_kernel(tc, x, scores, Wv, bv, Wo, bo, out):
             piece_mixw = big.tile([P, PIECE_GROUPS, HEADS, GROUP_POS, VIEWS], F32, tag="big")
             mix_weights[piece] = piece_mixw
 
-        def group_in_piece(grp):
-            c, b = chunk_and_scene(grp)
-            piece, part = divmod(c, PIECE_CHUNKS)
-            return piece, part * SCENES + b
-
-        def build_mix_weights(grp, heads):
-            piece, part = group_in_piece(grp)
-            c, b = chunk_and_scene(grp)
-            shape = [P, heads, GROUP_POS, VIEWS]
-            for h in range(0, HEADS, heads):
-                nc.vector.tensor_tensor(
-                    out=mix_weights[piece][:, part, h : h + heads],
-                    in0=weights_t[:, c, b, h : h + heads, :].unsqueeze(2).to_broadcast(shape),
-                    in1=block_mask[:].unsqueeze(1).to_broadcast(shape),
-                    op=MULT,
-                )
-
-        def spread_mix_weights(piece, positions):
+        def spread_mix_weights(piece, positions, on_vector):
             chunks = slice(piece * PIECE_CHUNKS, (piece + 1) * PIECE_CHUNKS)
             for s in positions:
-                nc.scalar.activation(
-                    out=mix_weights[piece][:, :, :, s, :],
-                    in_=weights_t[:, chunks].rearrange("p c b h i -> p (c b) h i"),
-                    func=COPY,
-                    scale=same_pos[:, s : s + 1],
-                )
+                columns = mix_weights[piece][:, :, :, s, :]
+                weights = weights_t[:, chunks].rearrange("p c b h i -> p (c b) h i")
+                own = same_pos[:, s : s + 1]
+                if on_vector:
+                    nc.vector.tensor_scalar(out=columns, in0=weights, scalar1=own, scalar2=None, op0=MULT)
+                else:
+                    nc.scalar.activation(out=columns, in_=weights, func=COPY, scale=own)
 
         def mix(grp):
-            piece, part = group_in_piece(grp)
+            c, b = chunk_and_scene(grp)
+            piece, chunk_in_piece = divmod(c, PIECE_CHUNKS)
+            part = chunk_in_piece * SCENES + b
             sums = []
             for g in range(PASSES):
                 acc = psum.tile([P, PACK, P], F32, tag="acc_mix")
@@ -446,10 +432,6 @@ def tile_crossviewattention_pa_kernel(tc, x, scores, Wv, bv, Wo, bo, out):
                 queue = nc.scalar if grp == GROUPS - 1 and half == 1 else nc.sync
                 queue.dma_start(out=group_rows(out, grp, half_cols(half)), in_=result[:])
 
-        def finish_group(grp):
-            second_projection(grp)
-            finish(grp)
-
         def is_group(grp):
             return 0 <= grp < GROUPS
 
@@ -457,98 +439,93 @@ def tile_crossviewattention_pa_kernel(tc, x, scores, Wv, bv, Wo, bo, out):
             slab, offset = divmod(grp, SLAB_GROUPS)
             return slab if offset == 0 and FIRST_SLAB <= slab < SLABS else None
 
-        WO_START = -2
-        SPREAD_BO_STEP = MOST_BEHIND_Y - 1
-        FINISH_STEP = [max(grp + BEHIND_Y, MOST_BEHIND_Y + grp // 2) for grp in range(GROUPS)]
+        def turn_step(grp):
+            late = grp < EARLY_GROUPS or (grp in PAIRED and grp % 2 == 0)
+            return grp + (2 if late else 1)
 
-        V, S = nc.vector.tensor_copy, nc.scalar.copy
-        FIRST_IN_LOOP = 1
+        def finish_step(grp):
+            return max(grp + BEHIND_Y, FIRST_FINISH + grp // 2)
+
+        on_vector, on_scalar = nc.vector.tensor_copy, nc.scalar.copy
         transpose_tokens(0)
-        regroup_wv(V, 0, 0)
+        regroup_wv(on_vector, 0, 0)
         quantise_tokens(0)
-        regroup_wv(S, 0, 1)
-        regroup_wv(V, 1, 0)
-        regroup_wv(S, 1, 1)
-        quantise_weights("wv", wv_codes, wv_scales, 0, 0)
-        quantise_weights("wv", wv_codes, wv_scales, 1, 0)
+        regroup_wv(on_scalar, 0, 1)
+        regroup_wv(on_vector, 1, 0)
+        regroup_wv(on_scalar, 1, 1)
+        for g in range(PASSES):
+            quantise_weights("wv", wv_codes, wv_scales, g, 0)
         softmax_shift(0)
-        regroup_wv(S, 0, 3)
+        regroup_wv(on_scalar, 0, 3)
         softmax_exp(0)
-        regroup_wv(V, 0, 2)
+        regroup_wv(on_vector, 0, 2)
         first_projection(0, 0)
-        regroup_wv(S, 1, 3)
-        regroup_wv(V, 1, 2)
+        regroup_wv(on_scalar, 1, 3)
+        regroup_wv(on_vector, 1, 2)
         softmax_normalise(0)
-        quantise_weights("wv", wv_codes, wv_scales, 0, 1)
-        quantise_weights("wv", wv_codes, wv_scales, 1, 1)
+        for g in range(PASSES):
+            quantise_weights("wv", wv_codes, wv_scales, g, 1)
         transpose_tokens(1)
         softmax_transpose(0)
         first_projection(0, 1)
-        spread_bias(0)
+        spread_bias()
         open_mix_weights(0)
-        build_mix_weights(0, HEADS // 2)
+        spread_mix_weights(0, range(GROUP_POS), on_vector=True)
 
         for step in range(FIRST_STEP, GROUPS):
-            piece = piece_that_starts_at(step + LEAD + 1)
-            if piece is not None and piece > 0:
-                softmax_exp(piece)
+            to_shift, to_exp, to_normalise, to_transpose = (
+                piece_that_starts_at(step + lead) for lead in (6, 5, 4, 3)
+            )
+            if to_exp is not None:
+                softmax_exp(to_exp)
+            for grp in range(GROUPS):
+                if turn_step(grp) == step - 1:
+                    quantise_mixed(grp)
             if is_group(step - 1):
                 round_mixed(step - 1)
-            if is_group(step - 2):
-                quantise_mixed(step - 2)
-            part = step - WO_START
-            if 1 < part <= PASSES * N_HALVES + 1:
-                half, g = divmod(part - 2, PASSES)
+            unit = step - (FIRST_FINISH - WO_LEAD)
+            if 0 <= unit - 2 < PASSES * N_HALVES:
+                half, g = divmod(unit - 2, PASSES)
                 quantise_weights("wo", wo_codes, wo_scales, g, half)
             for grp in range(GROUPS):
-                if FINISH_STEP[grp] == step:
+                if finish_step(grp) == step:
                     second_projection(grp)
                     finish(grp)
-            piece = piece_that_starts_at(step + LEAD)
-            if piece is not None:
-                softmax_normalise(piece)
-            if step + AHEAD_V + 2 < TURNED_BY_TENSOR:
-                transpose_tokens(step + AHEAD_V + 2)
-            if is_group(step - 1):
-                transpose_mixed(step - 1)
-            slab = slab_that_starts_at(step + AHEAD_V + 4)
+            if to_normalise is not None:
+                softmax_normalise(to_normalise)
+            if step + AHEAD_X < TURNED_BY_TENSOR:
+                transpose_tokens(step + AHEAD_X)
+            for grp in range(GROUPS):
+                if turn_step(grp) == step:
+                    transpose_mixed(grp)
+            if to_transpose is not None:
+                softmax_transpose(to_transpose)
+            slab = slab_that_starts_at(step + AHEAD_X + 2)
             if slab is not None:
                 order_slab(slab)
-            slab = slab_that_starts_at(step + AHEAD_V + 3)
+            slab = slab_that_starts_at(step + AHEAD_X + 1)
             if slab is not None:
                 turn_slab(slab)
-            if TURNED_BY_TENSOR <= step + AHEAD_V + 2 < GROUPS:
-                group_tokens(step + AHEAD_V + 2)
-            if is_group(step + AHEAD_V + 1):
-                quantise_tokens(step + AHEAD_V + 1)
-            piece = piece_that_starts_at(step + LEAD + 2)
-            if piece is not None and piece > 0:
-                softmax_shift(piece)
-            if 1 <= step + AHEAD_W < BY_GPSIMD:
-                if (step + AHEAD_W) % PIECE_GROUPS == 0:
-                    open_mix_weights((step + AHEAD_W) // PIECE_GROUPS)
-                build_mix_weights(step + AHEAD_W, HEADS)
-            piece, quarter = divmod(step + PIECE_GROUPS, PIECE_GROUPS)
-            if BY_GPSIMD <= piece * PIECE_GROUPS < GROUPS and quarter > 0:
-                if quarter == 1:
+            if TURNED_BY_TENSOR <= step + AHEAD_X < GROUPS:
+                group_tokens(step + AHEAD_X)
+            if is_group(step + AHEAD_X - 1):
+                quantise_tokens(step + AHEAD_X - 1)
+            if to_shift is not None:
+                softmax_shift(to_shift)
+            piece, third = divmod(step + PIECE_GROUPS - 1, PIECE_GROUPS)
+            if 0 < piece < PIECES and third < 3:
+                if third == 0:
                     open_mix_weights(piece)
-                spread_mix_weights(piece, range(quarter * 6 - 6, min(quarter * 6, GROUP_POS)))
-            if step == SPREAD_BO_STEP:
-                spread_bias(1)
-                store_bias(1, bo_all)
+                spread_mix_weights(piece, range(6 * third, min(6 * third + 6, GROUP_POS)), on_vector=False)
             if step == 0:
-                store_bias(0, bv_all)
+                store_bias()
             if is_group(step):
                 mix(step)
-            if FIRST_IN_LOOP <= step + AHEAD_V < GROUPS:
+            if 0 < step + AHEAD_V < GROUPS:
                 for half in range(N_HALVES):
                     first_projection(step + AHEAD_V, half)
-
-            piece = piece_that_starts_at(step + LEAD)
-            if piece is not None:
-                softmax_transpose(piece)
-            if 0 <= part < PASSES * N_HALVES:
-                half, g = divmod(part, PASSES)
+            if 0 <= unit < PASSES * N_HALVES:
+                half, g = divmod(unit, PASSES)
                 regroup_wo(g, half)
 
         last = GROUPS - 1

@@ -126,8 +126,8 @@ def tile_crossviewattention_pa_kernel(tc, x, scores, Wv, bv, Wo, bo, out):
                 out=score_raw[:, j, :], in_=scores[:, :, j, :, :].rearrange("b i h s -> (b i) h s")
             )
 
-        bias_rows = keep.tile([P, FEATURES], BF16)
-        nc.vector.memset(bias_rows[:].bitcast(U32), 0)
+        bias_rows = keep.tile([P, 2, FEATURES], BF16)
+        nc.vector.memset(bias_rows[:].rearrange("p k n -> p (k n)").bitcast(U32), 0)
         ones = keep.tile([P, P], BF16)
         nc.vector.memset(ones[:], 1.0)
         ident = keep.tile([P, P], F32)
@@ -135,7 +135,7 @@ def tile_crossviewattention_pa_kernel(tc, x, scores, Wv, bv, Wo, bo, out):
         warm = keep.tile([P, 1], F32)
         nc.vector.memset(warm[:], 0.0)
 
-        nc.gpsimd.dma_start(out=bias_rows[0:1, :], in_=bv.rearrange("(a n) -> a n", a=1))
+        nc.gpsimd.dma_start(out=bias_rows[0:1, 0, :], in_=bv.rearrange("(a n) -> a n", a=1))
         for j in range(SCALAR_LOADS):
             load_scores(j, nc.scalar)
             if j == 1:
@@ -144,6 +144,7 @@ def tile_crossviewattention_pa_kernel(tc, x, scores, Wv, bv, Wo, bo, out):
                     load_wv(g, 0)
         for j in range(SCALAR_LOADS, VIEWS):
             load_scores(j, nc.gpsimd)
+        nc.gpsimd.dma_start(out=bias_rows[0:1, 1, :], in_=bo.rearrange("(a n) -> a n", a=1))
         nc.scalar.activation(out=warm[:], in_=warm[:], func=EXP)
         for g in range(PASSES):
             load_wv(g, 1)
@@ -155,7 +156,6 @@ def tile_crossviewattention_pa_kernel(tc, x, scores, Wv, bv, Wo, bo, out):
             load_tokens(grp)
         for slab in range(FIRST_SLAB, SLABS):
             load_slab(slab)
-        nc.sync.dma_start(out=bo_all[:], in_=bo.partition_broadcast(P))
         same_pos = keep.tile([P, GROUP_POS], F32)
         nc.vector.tensor_reduce(
             out=same_pos[:], in_=ident[:].rearrange("p (s i) -> p s i", i=VIEWS), axis=INNERMOST, op=ADD
@@ -296,20 +296,20 @@ def tile_crossviewattention_pa_kernel(tc, x, scores, Wv, bv, Wo, bo, out):
 
         spread_sums = []
 
-        def spread_bias():
+        def spread_bias(k):
             spread = psum.tile([P, FEATURES], BF16, tag="acc_y")
             for half in range(N_HALVES):
                 nc.tensor.matmul(
                     out=spread[:, half_cols(half)],
                     lhsT=ones[:],
-                    rhs=bias_rows[:, half_cols(half)],
+                    rhs=bias_rows[:, k, half_cols(half)],
                     start=True,
                     stop=True,
                 )
             spread_sums.append(spread)
 
-        def store_bias():
-            nc.vector.tensor_copy(out=bv_all[:], in_=spread_sums[0][:])
+        def store_bias(k, bias_all):
+            nc.vector.tensor_copy(out=bias_all[:], in_=spread_sums[k][:])
 
         values = {}
         mix_weights = {}
@@ -468,7 +468,8 @@ def tile_crossviewattention_pa_kernel(tc, x, scores, Wv, bv, Wo, bo, out):
         transpose_tokens(1)
         softmax_transpose(0)
         first_projection(0, 1)
-        spread_bias()
+        spread_bias(0)
+        spread_bias(1)
         open_mix_weights(0)
         spread_mix_weights(0, range(GROUP_POS), on_vector=True)
 
@@ -518,7 +519,9 @@ def tile_crossviewattention_pa_kernel(tc, x, scores, Wv, bv, Wo, bo, out):
                     open_mix_weights(piece)
                 spread_mix_weights(piece, range(6 * third, min(6 * third + 6, GROUP_POS)), on_vector=False)
             if step == 0:
-                store_bias()
+                store_bias(0, bv_all)
+            if step == FIRST_FINISH - 1:
+                store_bias(1, bo_all)
             if is_group(step):
                 mix(step)
             if 0 < step + AHEAD_V < GROUPS:

from contextlib import ExitStack

import concourse.mybir as mybir
from concourse.masks import make_identity

F32 = mybir.dt.float32
BF16 = mybir.dt.bfloat16
U32 = mybir.dt.uint32
U8 = mybir.dt.uint8
FP8X4 = mybir.dt.float8_e4m3fn_x4
ADD = mybir.AluOpType.add
SUBTRACT = mybir.AluOpType.subtract
MULT = mybir.AluOpType.mult
MAX = mybir.AluOpType.max
INNERMOST = mybir.AxisListType.X
COPY = mybir.ActivationFunctionType.Copy
EXP = mybir.ActivationFunctionType.Exp

P = 128
SCENES, VIEWS, POSITIONS, FEATURES, HEADS = 2, 8, 128, 1024, 8
PACK = 4
K_PASS = P * PACK
PASSES = FEATURES // K_PASS
N_TILE = 512
N_HALVES = FEATURES // N_TILE
N_QUARTER = N_TILE // 2
GROUP_POS = P // VIEWS
CHUNKS = POSITIONS // GROUP_POS
GROUPS = SCENES * CHUNKS

PIECE_CHUNKS = 2
PIECE_GROUPS = PIECE_CHUNKS * SCENES
PIECE_POS = PIECE_CHUNKS * GROUP_POS
PIECES = CHUNKS // PIECE_CHUNKS

TURNED_BY_TENSOR = 8
SLAB_GROUPS = 2
SLABS = GROUPS // SLAB_GROUPS
FIRST_SLAB = TURNED_BY_TENSOR // SLAB_GROUPS
QUADS = 4
QUAD = P // QUADS
QUAD_FEATURES = K_PASS // QUADS

AHEAD_V = 2
AHEAD_X = AHEAD_V + 2
BEHIND_Y = 3
FIRST_FINISH = 4
WO_LEAD = 6
FIRST_STEP = -AHEAD_V
EARLY_GROUPS = 3
PAIRED = range(6, 14)
SCALAR_LOADS = 7

FLOPS = 2 * 2 * SCENES * VIEWS * POSITIONS * FEATURES * FEATURES + 2 * SCENES * VIEWS * VIEWS * POSITIONS * FEATURES


def tile_crossviewattention_pa_kernel(tc, x, scores, Wv, bv, Wo, bo, out):
    nc = tc.nc
    with ExitStack() as ctx:
        keep = ctx.enter_context(tc.tile_pool(name="keep", bufs=1))
        x_pool = ctx.enter_context(tc.tile_pool(name="x_pool", bufs=5))
        x_stage = ctx.enter_context(tc.tile_pool(name="x_stage", bufs=3))
        slab_stage = ctx.enter_context(tc.tile_pool(name="slab_stage", bufs=2))
        w_stage = ctx.enter_context(tc.tile_pool(name="w_stage", bufs=4))
        s_pool = ctx.enter_context(tc.tile_pool(name="s_pool", bufs=2))
        v_pool = ctx.enter_context(tc.tile_pool(name="v_pool", bufs=AHEAD_V + 2))
        big = ctx.enter_context(tc.tile_pool(name="big", bufs=3))
        m_pool = ctx.enter_context(tc.tile_pool(name="m_pool", bufs=5))
        y_pool = ctx.enter_context(tc.tile_pool(name="y_pool", bufs=6))
        psum = ctx.enter_context(tc.psum_pool(name="psum", bufs=2))
        ctx.enter_context(tc.manual_schedule())

        def chunk_and_scene(grp):
            piece, rest = divmod(grp, PIECE_GROUPS)
            b, part = divmod(rest, PIECE_CHUNKS)
            return piece * PIECE_CHUNKS + part, b

        def group_rows(dram, grp, cols):
            c, b = chunk_and_scene(grp)
            block = dram[b * VIEWS : (b + 1) * VIEWS, c * GROUP_POS : (c + 1) * GROUP_POS, cols]
            return block.rearrange("j s k -> s j k")

        def half_cols(half):
            return slice(half * N_TILE, (half + 1) * N_TILE)

        x_rows = keep.tile([P, TURNED_BY_TENSOR, FEATURES], BF16)
        x_slabs = keep.tile([P, SLABS - FIRST_SLAB, VIEWS, PASSES, QUAD_FEATURES], BF16)
        wv_raw = big.tile([P, PASSES, PACK, FEATURES], BF16, tag="big")
        wv_codes = keep.tile([P, PASSES, FEATURES], U32, align_bytes=64)
        wv_scales = keep.tile([P, PASSES, FEATURES], U8, align_bytes=64)
        wo_raw = big.tile([P, PASSES, PACK, FEATURES], BF16, tag="big")
        wo_codes = keep.tile([P, PASSES, FEATURES], U32, align_bytes=64)
        wo_scales = keep.tile([P, PASSES, FEATURES], U8, align_bytes=64)
        score_raw = keep.tile([P, VIEWS, POSITIONS], BF16)
        bv_all = keep.tile([P, FEATURES], BF16)
        bo_all = keep.tile([P, FEATURES], BF16)

        def load_tokens(grp):
            nc.sync.dma_start(out=x_rows[:, grp, :], in_=group_rows(x, grp, slice(0, FEATURES)))

        def load_slab(slab):
            piece, b = divmod(slab, SCENES)
            block = x[b * VIEWS : (b + 1) * VIEWS, piece * PIECE_POS : (piece + 1) * PIECE_POS, :]
            for g in range(PASSES):
                for a in range(QUADS):
                    first = g * K_PASS + a * QUAD_FEATURES
                    nc.sync.dma_start(
                        out=x_slabs[a * QUAD : (a + 1) * QUAD, slab - FIRST_SLAB, :, g, :],
                        in_=block[:, :, first : first + QUAD_FEATURES].rearrange("j r k -> r j k"),
                    )

        def load_wv(g, half):
            nc.sync.dma_start(
                out=wv_raw[:, g, :, half_cols(half)],
                in_=Wv[g * K_PASS : (g + 1) * K_PASS, half_cols(half)].rearrange("(p t) n -> p t n", t=PACK),
            )

        def load_wo(g):
            nc.sync.dma_start(
                out=wo_raw[:, g, :, :],
                in_=Wo[g * K_PASS : (g + 1) * K_PASS, :].rearrange("(p t) n -> p t n", t=PACK),
            )

        def load_scores(j, queue):
            queue.dma_start(
                out=score_raw[:, j, :], in_=scores[:, :, j, :, :].rearrange("b i h s -> (b i) h s")
            )

        bias_rows = keep.tile([P, 2, FEATURES], BF16)
        nc.vector.memset(bias_rows[:].rearrange("p k n -> p (k n)").bitcast(U32), 0)
        ones = keep.tile([P, P], BF16)
        nc.vector.memset(ones[:], 1.0)
        ident = keep.tile([P, P], F32)
        make_identity(nc, ident[:])
        warm = keep.tile([P, 1], F32)
        nc.vector.memset(warm[:], 0.0)

        nc.gpsimd.dma_start(out=bias_rows[0:1, 0, :], in_=bv.rearrange("(a n) -> a n", a=1))
        for j in range(SCALAR_LOADS):
            load_scores(j, nc.scalar)
            if j == 1:
                load_tokens(0)
                for g in range(PASSES):
                    load_wv(g, 0)
        for j in range(SCALAR_LOADS, VIEWS):
            load_scores(j, nc.gpsimd)
        nc.gpsimd.dma_start(out=bias_rows[0:1, 1, :], in_=bo.rearrange("(a n) -> a n", a=1))
        nc.scalar.activation(out=warm[:], in_=warm[:], func=EXP)
        for g in range(PASSES):
            load_wv(g, 1)
        for grp in range(1, 4):
            load_tokens(grp)
        for g in range(PASSES):
            load_wo(g)
        for grp in range(4, TURNED_BY_TENSOR):
            load_tokens(grp)
        for slab in range(FIRST_SLAB, SLABS):
            load_slab(slab)
        same_pos = keep.tile([P, GROUP_POS], F32)
        nc.vector.tensor_reduce(
            out=same_pos[:], in_=ident[:].rearrange("p (s i) -> p s i", i=VIEWS), axis=INNERMOST, op=ADD
        )

        grouped_weights = {}

        def regroup_weights(copy, name, raw, g, quarter):
            half, part = divmod(quarter, 2)
            key = (name, g, half)
            if key not in grouped_weights:
                grouped_w = w_stage.tile([P, N_TILE, PACK], BF16, align_bytes=64)
                grouped_weights[key] = grouped_w
            inner = slice(part * N_QUARTER, (part + 1) * N_QUARTER)
            outer = slice(quarter * N_QUARTER, (quarter + 1) * N_QUARTER)
            copy(
                out=grouped_weights[key][:, inner, :].rearrange("p (c i) t -> p c t i", i=4),
                in_=raw[:, g, :, outer].rearrange("p t (c i) -> p c t i", i=4),
            )

        def quantise_weights(name, codes, scales, g, half):
            nc.vector.quantize_mx(
                out=codes[:, g, half_cols(half)].bitcast(FP8X4),
                scales=scales[:, g, half_cols(half)],
                in_=grouped_weights[(name, g, half)][:].rearrange("p n t -> p (n t)"),
            )

        def regroup_wv(copy, g, quarter):
            regroup_weights(copy, "wv", wv_raw, g, quarter)

        def regroup_wo(g, half):
            regroup_weights(nc.vector.tensor_copy, "wo", wo_raw, g, 2 * half)
            regroup_weights(nc.scalar.copy, "wo", wo_raw, g, 2 * half + 1)

        grouped_tokens = {}
        token_codes = {}

        def transpose_tokens(grp):
            words = x_rows[:, grp, :].bitcast(F32)
            flipped = psum.tile([P, PACK, P], F32, tag="flip")
            for g in range(PASSES):
                for u in range(2):
                    nc.tensor.transpose(
                        flipped[:, 2 * g + u, :], words[:, 2 * P * g + u : 2 * P * (g + 1) : 2], ident[:]
                    )
            grouped_x = x_stage.tile([P, PASSES, P, PACK], BF16, align_bytes=64)
            nc.scalar.copy(
                out=grouped_x[:].bitcast(F32), in_=flipped[:].rearrange("p (g u) n -> p g n u", u=2)
            )
            grouped_tokens[grp] = grouped_x

        ordered_slabs = {}
        turned_slabs = {}

        def order_slab(slab):
            ordered = slab_stage.tile([P, VIEWS, PASSES, 2, QUAD], F32, align_bytes=64)
            words = x_slabs[:, slab - FIRST_SLAB].rearrange("p j g k -> p (j g k)").bitcast(F32)
            nc.scalar.copy(
                out=ordered[:].rearrange("p j g u i -> p (j g) u i"),
                in_=words.rearrange("p (b i u) -> p b u i", i=QUAD, u=2),
            )
            ordered_slabs[slab] = ordered

        def turn_slab(slab):
            turned = slab_stage.tile([P, VIEWS, PASSES, 2, QUAD], F32, align_bytes=64)
            nc.vector.transpose(
                out=turned[:].rearrange("p j g u r -> p (j g u r)"),
                in_=ordered_slabs[slab][:].rearrange("p j g u i -> p (j g u i)"),
            )
            turned_slabs[slab] = turned

        def group_tokens(grp):
            slab, part = divmod(grp, SLAB_GROUPS)
            grouped_x = x_stage.tile([P, PASSES, P, PACK], BF16, align_bytes=64)
            positions = slice(part * GROUP_POS, (part + 1) * GROUP_POS)
            for g in range(PASSES):
                nc.scalar.copy(
                    out=grouped_x[:, g, :, :].bitcast(F32).rearrange("p (s j) u -> p s j u", j=VIEWS),
                    in_=turned_slabs[slab][:, :, g, :, positions].rearrange("p j u s -> p s j u"),
                )
            grouped_tokens[grp] = grouped_x

        def quantise_tokens(grp):
            x_codes = x_pool.tile([P, PASSES * P], U32, align_bytes=64)
            x_scales = x_pool.tile([P, PASSES * P], U8, align_bytes=64)
            token_codes[grp] = (x_codes, x_scales)
            nc.vector.quantize_mx(
                out=x_codes[:].bitcast(FP8X4),
                scales=x_scales[:],
                in_=grouped_tokens[grp][:].rearrange("p g n t -> p (g n t)"),
            )

        weights_t = keep.tile([P, CHUNKS, SCENES, HEADS, VIEWS], F32)
        piece_shape = [P, PIECE_POS, VIEWS]
        exponents = {}
        piece_weights = {}

        def softmax_shift(piece):
            by_pos = score_raw[:, :, piece * PIECE_POS : (piece + 1) * PIECE_POS].rearrange("p j s -> p s j")
            top = s_pool.tile([P, PIECE_POS], F32)
            nc.vector.tensor_reduce(out=top[:], in_=by_pos, axis=INNERMOST, op=MAX)
            expd = s_pool.tile(piece_shape, F32)
            nc.vector.tensor_tensor(
                out=expd[:], in0=by_pos, in1=top[:].unsqueeze(2).to_broadcast(piece_shape), op=SUBTRACT
            )
            exponents[piece] = expd

        def softmax_exp(piece):
            nc.scalar.activation(out=exponents[piece][:], in_=exponents[piece][:], func=EXP)

        def softmax_normalise(piece):
            total = s_pool.tile([P, PIECE_POS], F32)
            nc.vector.tensor_reduce(out=total[:], in_=exponents[piece][:], axis=INNERMOST, op=ADD)
            inverse = s_pool.tile([P, PIECE_POS], F32)
            nc.vector.reciprocal(out=inverse[:], in_=total[:])
            weights = s_pool.tile([P, PIECE_CHUNKS, P], F32)
            nc.vector.tensor_tensor(
                out=weights[:].rearrange("p c (s j) -> p (c s) j", j=VIEWS),
                in0=exponents[piece][:],
                in1=inverse[:].unsqueeze(2).to_broadcast(piece_shape),
                op=MULT,
            )
            piece_weights[piece] = weights

        def softmax_transpose(piece):
            flipped = psum.tile([P, PACK, P], F32, tag="flip")
            for c in range(PIECE_CHUNKS):
                nc.tensor.transpose(flipped[:, c, :], piece_weights[piece][:, c, :], ident[:])
            chunks = slice(piece * PIECE_CHUNKS, (piece + 1) * PIECE_CHUNKS)
            nc.scalar.copy(
                out=weights_t[:, chunks].rearrange("p c b h i -> p (c b) h i"),
                in_=flipped[:, 0:PIECE_CHUNKS, :].rearrange("p c (b i h) -> p (c b) h i", b=SCENES, i=VIEWS),
            )

        def piece_that_starts_at(grp):
            piece, offset = divmod(grp, PIECE_GROUPS)
            return piece if offset == 0 and 0 < piece < PIECES else None

        spread_sums = []

        def spread_bias(k):
            spread = psum.tile([P, FEATURES], BF16, tag="acc_y")
            for half in range(N_HALVES):
                nc.tensor.matmul(
                    out=spread[:, half_cols(half)],
                    lhsT=ones[:],
                    rhs=bias_rows[:, k, half_cols(half)],
                    start=True,
                    stop=True,
                )
            spread_sums.append(spread)

        def store_bias(k, bias_all):
            nc.vector.tensor_copy(out=bias_all[:], in_=spread_sums[k][:])

        values = {}
        mix_weights = {}
        mix_sums = {}
        mixed_tokens = {}
        grouped_mixed = {}
        mixed_codes = {}
        out_sums = {}

        def first_projection(grp, half):
            if half == 0:
                v_rows = v_pool.tile([P, FEATURES], F32)
                values[grp] = v_rows
            x_codes, x_scales = token_codes[grp]
            acc = psum.tile([P, N_TILE], F32, tag="acc_v")
            for g in range(PASSES):
                toks = slice(g * P, (g + 1) * P)
                nc.tensor.matmul_mx(
                    out=acc[:],
                    lhsT=x_codes[:, toks].bitcast(FP8X4),
                    lhsT_scale=x_scales[:, toks],
                    rhs=wv_codes[:, g, half_cols(half)].bitcast(FP8X4),
                    rhs_scale=wv_scales[:, g, half_cols(half)],
                    start=(g == 0),
                    stop=(g == PASSES - 1),
                )
            nc.scalar.copy(out=values[grp][:, half_cols(half)], in_=acc[:])

        def open_mix_weights(piece):
            piece_mixw = big.tile([P, PIECE_GROUPS, HEADS, GROUP_POS, VIEWS], F32, tag="big")
            mix_weights[piece] = piece_mixw

        def spread_mix_weights(piece, positions, on_vector):
            chunks = slice(piece * PIECE_CHUNKS, (piece + 1) * PIECE_CHUNKS)
            for s in positions:
                columns = mix_weights[piece][:, :, :, s, :]
                weights = weights_t[:, chunks].rearrange("p c b h i -> p (c b) h i")
                own = same_pos[:, s : s + 1]
                if on_vector:
                    nc.vector.tensor_scalar(out=columns, in0=weights, scalar1=own, scalar2=None, op0=MULT)
                else:
                    nc.scalar.activation(out=columns, in_=weights, func=COPY, scale=own)

        def mix(grp):
            c, b = chunk_and_scene(grp)
            piece, chunk_in_piece = divmod(c, PIECE_CHUNKS)
            part = chunk_in_piece * SCENES + b
            sums = []
            for g in range(PASSES):
                acc = psum.tile([P, PACK, P], F32, tag="acc_mix")
                for t in range(PACK):
                    h = g * PACK + t
                    nc.tensor.matmul(
                        out=acc[:, t, :],
                        lhsT=mix_weights[piece][:, part, h, :, :].rearrange("p s i -> p (s i)"),
                        rhs=values[grp][:, h * P : (h + 1) * P],
                        start=True,
                        stop=True,
                    )
                sums.append(acc)
            mix_sums[grp] = sums

        def round_mixed(grp):
            mixed = m_pool.tile([P, PASSES, 2, P, 2], BF16, align_bytes=64)
            for g in range(PASSES):
                nc.vector.tensor_tensor(
                    out=mixed[:, g],
                    in0=mix_sums[grp][g][:].rearrange("p t f -> p (t f)").rearrange("p (q u e) -> p u q e", u=2, e=2),
                    in1=bv_all[:, g * K_PASS : (g + 1) * K_PASS].rearrange("p (q u e) -> p u q e", u=2, e=2),
                    op=ADD,
                )
            mixed_tokens[grp] = mixed

        def transpose_mixed(grp):
            words = mixed_tokens[grp][:].rearrange("p g u q e -> p (g u q e)").bitcast(F32)
            flipped = psum.tile([P, PACK, P], F32, tag="flip")
            for c in range(PACK):
                nc.tensor.transpose(flipped[:, c, :], words[:, c * P : (c + 1) * P], ident[:])
            grouped_m = m_pool.tile([P, PASSES, P, PACK], BF16, align_bytes=64)
            nc.scalar.copy(
                out=grouped_m[:].bitcast(F32), in_=flipped[:].rearrange("p (g u) n -> p g n u", u=2)
            )
            grouped_mixed[grp] = grouped_m

        def quantise_mixed(grp):
            m_codes = m_pool.tile([P, PASSES * P], U32, align_bytes=64)
            m_scales = m_pool.tile([P, PASSES * P], U8, align_bytes=64)
            nc.vector.quantize_mx(
                out=m_codes[:].bitcast(FP8X4),
                scales=m_scales[:],
                in_=grouped_mixed[grp][:].rearrange("p g n t -> p (g n t)"),
            )
            mixed_codes[grp] = (m_codes, m_scales)

        def second_projection(grp):
            m_codes, m_scales = mixed_codes[grp]
            sums = []
            for half in range(N_HALVES):
                acc = psum.tile([P, N_TILE], F32, tag="acc_v" if grp == GROUPS - 2 else "acc_y")
                for g in range(PASSES):
                    toks = slice(g * P, (g + 1) * P)
                    nc.tensor.matmul_mx(
                        out=acc[:],
                        lhsT=m_codes[:, toks].bitcast(FP8X4),
                        lhsT_scale=m_scales[:, toks],
                        rhs=wo_codes[:, g, half_cols(half)].bitcast(FP8X4),
                        rhs_scale=wo_scales[:, g, half_cols(half)],
                        start=(g == 0),
                        stop=(g == PASSES - 1),
                    )
                sums.append(acc)
            out_sums[grp] = sums

        def finish(grp):
            for half in range(N_HALVES):
                result = y_pool.tile([P, N_TILE], F32)
                nc.vector.tensor_tensor(
                    out=result[:], in0=out_sums[grp][half][:], in1=bo_all[:, half_cols(half)], op=ADD
                )
                queue = nc.scalar if grp == GROUPS - 1 and half == 1 else nc.sync
                queue.dma_start(out=group_rows(out, grp, half_cols(half)), in_=result[:])

        def is_group(grp):
            return 0 <= grp < GROUPS

        def slab_that_starts_at(grp):
            slab, offset = divmod(grp, SLAB_GROUPS)
            return slab if offset == 0 and FIRST_SLAB <= slab < SLABS else None

        def turn_step(grp):
            late = grp < EARLY_GROUPS or (grp in PAIRED and grp % 2 == 0)
            return grp + (2 if late else 1)

        def finish_step(grp):
            return max(grp + BEHIND_Y, FIRST_FINISH + grp // 2)

        on_vector, on_scalar = nc.vector.tensor_copy, nc.scalar.copy
        transpose_tokens(0)
        regroup_wv(on_vector, 0, 0)
        quantise_tokens(0)
        regroup_wv(on_scalar, 0, 1)
        regroup_wv(on_vector, 1, 0)
        regroup_wv(on_scalar, 1, 1)
        for g in range(PASSES):
            quantise_weights("wv", wv_codes, wv_scales, g, 0)
        softmax_shift(0)
        regroup_wv(on_scalar, 0, 3)
        softmax_exp(0)
        regroup_wv(on_vector, 0, 2)
        first_projection(0, 0)
        regroup_wv(on_scalar, 1, 3)
        regroup_wv(on_vector, 1, 2)
        softmax_normalise(0)
        for g in range(PASSES):
            quantise_weights("wv", wv_codes, wv_scales, g, 1)
        transpose_tokens(1)
        softmax_transpose(0)
        first_projection(0, 1)
        spread_bias(0)
        spread_bias(1)
        open_mix_weights(0)
        spread_mix_weights(0, range(GROUP_POS), on_vector=True)

        for step in range(FIRST_STEP, GROUPS):
            to_shift, to_exp, to_normalise, to_transpose = (
                piece_that_starts_at(step + lead) for lead in (6, 5, 4, 3)
            )
            if to_exp is not None:
                softmax_exp(to_exp)
            for grp in range(GROUPS):
                if turn_step(grp) == step - 1:
                    quantise_mixed(grp)
            if is_group(step - 1):
                round_mixed(step - 1)
            unit = step - (FIRST_FINISH - WO_LEAD)
            if 0 <= unit - 2 < PASSES * N_HALVES:
                half, g = divmod(unit - 2, PASSES)
                quantise_weights("wo", wo_codes, wo_scales, g, half)
            for grp in range(GROUPS):
                if finish_step(grp) == step:
                    second_projection(grp)
                    finish(grp)
            if to_normalise is not None:
                softmax_normalise(to_normalise)
            if step + AHEAD_X < TURNED_BY_TENSOR:
                transpose_tokens(step + AHEAD_X)
            for grp in range(GROUPS):
                if turn_step(grp) == step:
                    transpose_mixed(grp)
            if to_transpose is not None:
                softmax_transpose(to_transpose)
            slab = slab_that_starts_at(step + AHEAD_X + 2)
            if slab is not None:
                order_slab(slab)
            slab = slab_that_starts_at(step + AHEAD_X + 1)
            if slab is not None:
                turn_slab(slab)
            if TURNED_BY_TENSOR <= step + AHEAD_X < GROUPS:
                group_tokens(step + AHEAD_X)
            if is_group(step + AHEAD_X - 1):
                quantise_tokens(step + AHEAD_X - 1)
            if to_shift is not None:
                softmax_shift(to_shift)
            piece, third = divmod(step + PIECE_GROUPS - 1, PIECE_GROUPS)
            if 0 < piece < PIECES and third < 3:
                if third == 0:
                    open_mix_weights(piece)
                spread_mix_weights(piece, range(6 * third, min(6 * third + 6, GROUP_POS)), on_vector=False)
            if step == 0:
                store_bias(0, bv_all)
            if step == FIRST_FINISH - 1:
                store_bias(1, bo_all)
            if is_group(step):
                mix(step)
            if 0 < step + AHEAD_V < GROUPS:
                for half in range(N_HALVES):
                    first_projection(step + AHEAD_V, half)
            if 0 <= unit < PASSES * N_HALVES:
                half, g = divmod(unit, PASSES)
                regroup_wo(g, half)

        last = GROUPS - 1
        round_mixed(last)
        quantise_mixed(last - 1)
        second_projection(last - 2)
        transpose_mixed(last)
        finish(last - 2)
        second_projection(last - 1)
        quantise_mixed(last)
        finish(last - 1)
        second_projection(last)
        finish(last)
